import numpy as np
import ml_dtypes


def mxq(x, axis, fmt="e4m3"):
    dtype, down = {"e4m3": (ml_dtypes.float8_e4m3fn, 7), "e5m2": (ml_dtypes.float8_e5m2, 14)}[fmt]
    v = np.moveaxis(np.asarray(x, np.float32).astype(ml_dtypes.bfloat16).astype(np.float64), axis, -1)
    blocks = v.reshape(v.shape[:-1] + (-1, 32))
    amax = np.abs(blocks).max(-1, keepdims=True)
    byte = np.maximum(np.where(amax > 0, np.frexp(amax)[1] - 1 + 127, 0) - down, 1)
    scale = np.exp2(byte - 127.0)
    codes = (blocks / scale).astype(np.float32).astype(dtype).astype(np.float64)
    return np.moveaxis((codes * scale).reshape(v.shape), -1, axis)


WIDE = False


def mx_kscale(k):
    if not WIDE:
        return np.ones(k)
    levels = np.array([10, -10, 5, -5, 0])
    a = np.random.permutation(np.resize(levels, k // 512 * 4)).reshape(k // 512, 4)
    idx = np.arange(k)
    return np.exp2(a[idx // 512, idx % 128 // 32])


BF16 = ml_dtypes.bfloat16


def bf(x):
    return np.asarray(x, np.float32).astype(BF16)


def f64(x):
    return np.asarray(x).astype(np.float64)


E2M1 = np.array([0.0, 0.5, 1.0, 1.5, 2.0, 3.0, 4.0, 6.0, -0.0, -0.5, -1.0, -1.5, -2.0, -3.0, -4.0, -6.0])


def pack_weight(w, fmt):
    k, n = w.shape
    w = f64(bf(w)).reshape(k // 32, 32, n)
    amax = np.abs(w).max(1)
    if fmt == "e4m3":
        byte = np.frexp(amax)[1] - 1 + 127 - 7
    else:
        mant, ex = np.frexp(amax / 6.0)
        byte = np.where(mant > 0.5, ex, ex - 1) + 127
    byte = np.clip(np.where(amax > 0, byte, 1), 1, 254)
    scaled = (w * np.exp2(127.0 - byte)[:, None, :]).reshape(k, n).astype(np.float32)
    by_word = np.ascontiguousarray(scaled.reshape(k // 512, 128, 4, n).transpose(0, 1, 3, 2))
    if fmt == "e4m3":
        words = by_word.astype(ml_dtypes.float8_e4m3fn).view(np.uint8)
    else:
        c = by_word.astype(ml_dtypes.float4_e2m1fn).view(np.uint8) & 0xF
        words = c[..., 0::2] | (c[..., 1::2] << 4)
    return np.ascontiguousarray(words), np.ascontiguousarray(byte.astype(np.uint8).reshape(k // 512, 16, n))


def unpack_weight(words, scales, fmt):
    g, p, n, _ = words.shape
    if fmt == "e4m3":
        vals = np.ascontiguousarray(words).view(ml_dtypes.float8_e4m3fn).astype(np.float64)
    else:
        nib = np.empty((g, p, n, 4), np.uint8)
        nib[..., 0::2] = words & 0xF
        nib[..., 1::2] = words >> 4
        vals = E2M1[nib]
    vals = vals * np.repeat(np.exp2(scales.astype(np.float64) - 127.0), 8, axis=1)[..., None]
    return vals.transpose(0, 1, 3, 2).reshape(g * 512, n)


B, S, P, F, O, DEG, R = 2, 512, 2, 512, 512, 16, 4
OC = O + O + O
FMT = "e4m3"


def rows(scale):
    return np.random.standard_normal((B, S, P, F)) * np.exp(0.4 * np.random.standard_normal((B, S, P, 1))) * scale


def setup_inputs():
    s = mx_kscale(F)
    x = bf(rows(1.0) * s)
    nb = bf(rows(1.0 / np.sqrt(DEG)) * s)
    mu = bf(rows(1.0) * s)
    wx_words, wx_scales = pack_weight((np.random.standard_normal((O, F)) / np.sqrt(F) / s).T, FMT)
    wx_b = bf(0.1 * np.random.standard_normal(O))
    wn_words, wn_scales = pack_weight((np.random.standard_normal((O, F)) / np.sqrt(F) / s).T, FMT)
    wn_b = bf(0.1 * np.random.standard_normal(O))
    wr_words, wr_scales = pack_weight((np.random.standard_normal((O, F)) / np.sqrt(F) / s).T, FMT)
    wr_b = bf(0.1 * np.random.standard_normal(O))
    return {"x": x, "nb": nb, "mu": mu,
            "Wx_w_words": wx_words, "Wx_w_scales": wx_scales, "Wx_b": wx_b,
            "Wn_w_words": wn_words, "Wn_w_scales": wn_scales, "Wn_b": wn_b,
            "Wr_w_words": wr_words, "Wr_w_scales": wr_scales, "Wr_b": wr_b,
            "bn_gamma": bf(1.0 + 0.1 * np.random.standard_normal(OC)), "bn_beta": bf(0.1 * np.random.standard_normal(OC))}


def lin(x, words, scales, b):
    return (mxq(x, 3, "e4m3") @ unpack_weight(words, scales, FMT)) + b


def reference(x, nb, mu, Wx_w_words, Wx_w_scales, Wx_b, Wn_w_words, Wn_w_scales, Wn_b, Wr_w_words, Wr_w_scales, Wr_b, bn_gamma, bn_beta):
    h = np.concatenate([lin(f64(x), Wx_w_words, Wx_w_scales, f64(Wx_b)), lin(f64(nb), Wn_w_words, Wn_w_scales, f64(Wn_b)), lin(f64(mu), Wr_w_words, Wr_w_scales, f64(Wr_b))], axis=-1)
    n = np.maximum(np.sqrt((h ** 2).sum(3, keepdims=True)), 1e-12)
    r = np.maximum(h / n, 0.0)
    m = r.mean(axis=(0, 1, 2))
    v = r.var(axis=(0, 1, 2))
    return (r - m) / np.sqrt(v + 1e-5) * f64(bn_gamma) + f64(bn_beta)

@@ -1,0 +1,298 @@
+import concourse.mybir as mybir
+from concourse.masks import make_identity
+
+F32 = mybir.dt.float32
+BF16 = mybir.dt.bfloat16
+I32 = mybir.dt.int32
+U32 = mybir.dt.uint32
+U8 = mybir.dt.uint8
+FP8X4 = mybir.dt.float8_e4m3fn_x4
+ALU = mybir.AluOpType
+ACT = mybir.ActivationFunctionType
+AXIS = mybir.AxisListType
+
+P = 128
+ROWS = 2048
+K = 512
+STREAMS = 3
+STREAM_CHANNELS = 512
+CHANNELS = STREAMS * STREAM_CHANNELS
+BLOCKS = CHANNELS // P
+STREAM_BLOCKS = STREAM_CHANNELS // P
+ROW_TILES = ROWS // P
+GROUP_TILES = 4
+GROUP_ROWS = GROUP_TILES * P
+GROUPS = ROW_TILES // GROUP_TILES
+TILES = GROUPS * BLOCKS
+OPERANDS = GROUPS * STREAMS
+HALF_TILES = GROUP_TILES // 2
+HALVES = 2 * OPERANDS
+SCALE_ROWS = K // 32
+NORM_FLOOR = 1e-12
+BN_EPS = 1e-5
+
+HALVES_AHEAD = 3
+SUM_LAG = 3
+NORM_STAGES = 4
+APPLY_LAG = BLOCKS + SUM_LAG + NORM_STAGES
+
+FLOPS = 2 * ROWS * K * CHANNELS
+
+
+def tile_batchedgraphsagemean1_pb_kernel(
+    tc,
+    x,
+    nb,
+    mu,
+    Wx_w_words,
+    Wx_w_scales,
+    Wx_b,
+    Wn_w_words,
+    Wn_w_scales,
+    Wn_b,
+    Wr_w_words,
+    Wr_w_scales,
+    Wr_b,
+    bn_gamma,
+    bn_beta,
+    out,
+):
+    nc = tc.nc
+    streams = [src.flatten_outer_dims().rearrange("(p n) k -> p n k", n=ROW_TILES) for src in (x, nb, mu)]
+    weight_words = [Wx_w_words, Wn_w_words, Wr_w_words]
+    weight_scales = [Wx_w_scales, Wn_w_scales, Wr_w_scales]
+    out_rows = out.flatten_outer_dims().rearrange("(p n) c -> p n c", n=ROW_TILES)
+
+    with tc.tile_pool(name="keep", bufs=1) as keep, tc.tile_pool(name="work", bufs=2) as work, tc.manual_schedule():
+        ident = keep.tile([P, P], F32)
+        make_identity(nc, ident[:])
+        ones_col = keep.tile([P, 1], F32)
+        nc.vector.memset(ones_col[:], 1.0)
+
+        w_codes = keep.tile([P, STREAMS, STREAM_CHANNELS], U32, align_bytes=64)
+        w_planes = keep.tile([P, STREAMS, STREAM_CHANNELS], U8, align_bytes=64)
+        nc.vector.memset(w_planes[:].bitcast(I32), 0)
+
+        vec_rows = keep.tile([P, P], BF16)
+        nc.vector.memset(vec_rows[:], 0.0)
+        first_row = 0
+        for vec in (Wx_b, Wn_b, Wr_b, bn_gamma, bn_beta):
+            n_rows = vec.shape[0] // P
+            nc.scalar.dma_start(
+                out=vec_rows[first_row : first_row + n_rows, :], in_=vec.rearrange("(r c) -> r c", c=P)
+            )
+            first_row += n_rows
+
+        table_warm = keep.tile([P, 1], F32)
+        nc.scalar.activation(out=table_warm[:], in_=ones_col[:], func=ACT.Sqrt)
+
+        x_raw = keep.tile([P, STREAMS, ROW_TILES, K], BF16)
+
+        def load_half(q):
+            g, s, half = q // (2 * STREAMS), q // 2 % STREAMS, q % 2
+            first = g * GROUP_TILES + half * HALF_TILES
+            nc.sync.dma_start(
+                out=x_raw[:, s, first : first + HALF_TILES, :], in_=streams[s][:, first : first + HALF_TILES, :]
+            )
+
+        for s in range(STREAMS):
+            load_half(2 * s)
+            load_half(2 * s + 1)
+            nc.sync.dma_start(
+                out=w_codes[:, s, :].bitcast(I32),
+                in_=weight_words[s][0].rearrange("p n t -> p (n t)").bitcast(I32),
+            )
+            for quadrant in range(SCALE_ROWS // 4):
+                nc.sync.dma_start(
+                    out=w_planes[32 * quadrant : 32 * quadrant + 4, s, :].bitcast(I32),
+                    in_=weight_scales[s][0, 4 * quadrant : 4 * quadrant + 4, :].bitcast(I32),
+                )
+        for q in range(2 * STREAMS, HALVES):
+            load_half(q)
+
+        h_all = keep.tile([P, GROUPS, BLOCKS, GROUP_ROWS], F32)
+        sum_r = keep.tile([P, BLOCKS, GROUPS], F32)
+        sum_rr = keep.tile([P, BLOCKS, GROUPS], F32)
+        vec_cols = keep.tile([P, 3 * BLOCKS], F32)
+        bias = vec_cols[:, 0:BLOCKS]
+        gamma = vec_cols[:, BLOCKS : 2 * BLOCKS]
+        beta = vec_cols[:, 2 * BLOCKS : 3 * BLOCKS]
+
+        with tc.psum_pool(name="psum_front", bufs=1) as psum:
+            grouped = {}
+            operands = {}
+            squares = {}
+            square_sums = {}
+            chain = {}
+            spread = {}
+
+            def transpose_vectors():
+                vec_f32 = keep.tile([P, P], F32)
+                nc.vector.tensor_copy(out=vec_f32[:], in_=vec_rows[:])
+                vec_ps = psum.tile([P, P], F32, tag="xt", bufs=2)
+                nc.tensor.transpose(vec_ps[:], vec_f32[:], ident[:])
+                nc.vector.tensor_copy(out=vec_cols[:], in_=vec_ps[:, 0 : 3 * BLOCKS])
+
+            def transpose_half(q):
+                m, half = q // 2, q % 2
+                g, s = m // STREAMS, m % STREAMS
+                if half == 0:
+                    grouped[m] = work.tile([P, GROUP_ROWS, 2], F32, name="grouped", bufs=3, align_bytes=64)
+                xt = psum.tile([P, 2, HALF_TILES * P], F32, tag="xt", bufs=2)
+                for i in range(HALF_TILES):
+                    words = x_raw[:, s, g * GROUP_TILES + half * HALF_TILES + i, :].bitcast(F32)
+                    for u in range(2):
+                        nc.tensor.transpose(xt[:, u, i * P : (i + 1) * P], words[:, u : K // 2 : 2], ident[:])
+                rows = slice(half * HALF_TILES * P, (half + 1) * HALF_TILES * P)
+                nc.scalar.copy(out=grouped[m][:, rows, :], in_=xt[:].rearrange("p u r -> p r u"))
+
+            def quantise(m):
+                codes = work.tile([P, GROUP_ROWS], U32, tag="codes", bufs=2 * STREAMS, align_bytes=64)
+                plane = work.tile([P, GROUP_ROWS], U8, tag="plane", bufs=2 * STREAMS, align_bytes=64)
+                nc.vector.quantize_mx(
+                    out=codes[:].bitcast(FP8X4),
+                    scales=plane[:],
+                    in_=grouped[m][:].rearrange("p r u -> p (r u)").bitcast(BF16),
+                )
+                operands[m] = (codes, plane)
+
+            def project(i):
+                g, c = i // BLOCKS, i % BLOCKS
+                s = c // STREAM_BLOCKS
+                cols = slice((c % STREAM_BLOCKS) * P, (c % STREAM_BLOCKS + 1) * P)
+                codes, plane = operands[g * STREAMS + s]
+                acc = psum.tile([P, GROUP_ROWS], F32, tag="acc", bufs=3)
+                nc.tensor.matmul_mx(
+                    out=acc[:],
+                    lhsT=w_codes[:, s, cols].bitcast(FP8X4),
+                    lhsT_scale=w_planes[:, s, cols],
+                    rhs=codes[:].bitcast(FP8X4),
+                    rhs_scale=plane[:],
+                    start=True,
+                    stop=True,
+                )
+                nc.vector.tensor_scalar_add(out=h_all[:, g, c, :], in0=acc[:], scalar1=bias[:, c : c + 1])
+                squares[i] = work.tile([P, GROUP_ROWS], F32, name="squares", bufs=SUM_LAG + 2)
+                nc.scalar.activation(out=squares[i][:], in_=h_all[:, g, c, :], func=ACT.Square)
+
+            def sum_squares(i):
+                g, c = i // BLOCKS, i % BLOCKS
+                if c == 0:
+                    square_sums[g] = psum.tile([P, GROUP_TILES, BLOCKS], F32, name="square_sums", bufs=1)
+                for t in range(GROUP_TILES):
+                    nc.tensor.matmul(
+                        out=square_sums[g][:, t, c : c + 1],
+                        lhsT=squares[i][:, t * P : (t + 1) * P],
+                        rhs=ones_col[:],
+                        start=True,
+                        stop=True,
+                    )
+
+            def norm_stage(g, stage):
+                if stage == 0:
+                    chain[g] = [work.tile([P, GROUP_TILES], F32, name="chain%d" % n) for n in range(4)]
+                total, floored, norm, inv_norm = chain[g]
+                if stage == 0:
+                    nc.vector.tensor_reduce(out=total[:], in_=square_sums[g][:], axis=AXIS.X, op=ALU.add)
+                    nc.vector.tensor_scalar_max(out=floored[:], in0=total[:], scalar1=NORM_FLOOR * NORM_FLOOR)
+                if stage == 1:
+                    nc.scalar.activation(out=norm[:], in_=floored[:], func=ACT.Sqrt)
+                if stage == 2:
+                    nc.vector.reciprocal(out=inv_norm[:], in_=norm[:])
+                if stage == 3:
+                    spread[g] = psum.tile([P, GROUP_ROWS], F32, name="spread", bufs=2)
+                    for t in range(GROUP_TILES):
+                        nc.tensor.matmul(
+                            out=spread[g][:, t * P : (t + 1) * P],
+                            lhsT=inv_norm[:, t : t + 1].to_broadcast([P, P]),
+                            rhs=ident[:],
+                            start=True,
+                            stop=True,
+                        )
+
+            def normalise(i):
+                g, c = i // BLOCKS, i % BLOCKS
+                r = h_all[:, g, c, :]
+                nc.vector.scalar_tensor_tensor(
+                    out=r,
+                    in0=r,
+                    scalar=0.0,
+                    in1=spread[g][:],
+                    op0=ALU.max,
+                    op1=ALU.mult,
+                    accum_out=sum_r[:, c, g : g + 1],
+                )
+                unread = work.tile([P, GROUP_ROWS], F32, tag="unread", bufs=3)
+                nc.scalar.activation(out=unread[:], in_=r, func=ACT.Square, accum_out=sum_rr[:, c, g : g + 1])
+
+            transpose_half(0)
+            transpose_vectors()
+            for q in range(1, HALVES_AHEAD):
+                transpose_half(q)
+                if q % 2 == 1:
+                    quantise(q // 2)
+
+            for step in range(TILES + APPLY_LAG):
+                g, stage = divmod(step - BLOCKS - SUM_LAG, BLOCKS)
+                if 0 <= g < GROUPS and stage < NORM_STAGES:
+                    norm_stage(g, stage)
+                q = step // 2 + HALVES_AHEAD
+                if q < HALVES and step % 2 == 0:
+                    transpose_half(q)
+                if q < HALVES and step % 2 == 1 and q % 2 == 1:
+                    quantise(q // 2)
+                if step < TILES:
+                    project(step)
+                if 0 <= step - SUM_LAG < TILES:
+                    sum_squares(step - SUM_LAG)
+                if 0 <= step - APPLY_LAG:
+                    normalise(step - APPLY_LAG)
+
+        def small(name):
+            return keep.tile([P, BLOCKS], F32, name=name)
+
+        total_r, total_rr, mean, mean_sq, second = small("total_r"), small("total_rr"), small("mean"), small("mean_sq"), small("second")
+        var_eps, std, inv_std, gain, mean_gain, shift = small("var_eps"), small("std"), small("inv_std"), small("gain"), small("mean_gain"), small("shift")
+        nc.vector.tensor_reduce(out=total_r[:], in_=sum_r[:], axis=AXIS.X, op=ALU.add)
+        nc.vector.tensor_scalar_mul(out=mean[:], in0=total_r[:], scalar1=1.0 / ROWS)
+        nc.vector.tensor_mul(out=mean_sq[:], in0=mean[:], in1=mean[:])
+        nc.vector.tensor_reduce(out=total_rr[:], in_=sum_rr[:], axis=AXIS.X, op=ALU.add)
+        nc.vector.tensor_scalar(
+            out=second[:], in0=total_rr[:], scalar1=1.0 / ROWS, scalar2=BN_EPS, op0=ALU.mult, op1=ALU.add
+        )
+        nc.vector.tensor_sub(out=var_eps[:], in0=second[:], in1=mean_sq[:])
+        nc.scalar.activation(out=std[:], in_=var_eps[:], func=ACT.Sqrt)
+        nc.vector.reciprocal(out=inv_std[:], in_=std[:])
+        nc.vector.tensor_mul(out=gain[:], in0=gamma, in1=inv_std[:])
+        nc.vector.tensor_mul(out=mean_gain[:], in0=mean[:], in1=gain[:])
+        nc.vector.tensor_sub(out=shift[:], in0=beta, in1=mean_gain[:])
+
+        def scale_and_shift(g, c):
+            y = h_all[:, g, c, :]
+            nc.vector.tensor_scalar(
+                out=y, in0=y, scalar1=gain[:, c : c + 1], scalar2=shift[:, c : c + 1], op0=ALU.mult, op1=ALU.add
+            )
+
+        with tc.psum_pool(name="psum_back", bufs=6) as psum:
+            for c in range(BLOCKS):
+                scale_and_shift(0, c)
+            for g in range(GROUPS):
+                for t in range(GROUP_TILES):
+                    if g + 1 < GROUPS:
+                        for c in range(t * BLOCKS // GROUP_TILES, (t + 1) * BLOCKS // GROUP_TILES):
+                            scale_and_shift(g + 1, c)
+                    row_major = work.tile([P, CHANNELS], F32, tag="row_major", bufs=4)
+                    for s in range(STREAMS):
+                        yt = psum.tile([P, STREAM_CHANNELS], F32, tag="yt")
+                        for j in range(STREAM_BLOCKS):
+                            nc.tensor.transpose(
+                                yt[:, j * P : (j + 1) * P],
+                                h_all[:, g, s * STREAM_BLOCKS + j, t * P : (t + 1) * P],
+                                ident[:],
+                            )
+                        landing = row_major[:, s * STREAM_CHANNELS : (s + 1) * STREAM_CHANNELS]
+                        if s == 0:
+                            nc.vector.tensor_copy(out=landing, in_=yt[:])
+                        else:
+                            nc.scalar.copy(out=landing, in_=yt[:])
+                    nc.sync.dma_start(out=out_rows[:, g * GROUP_TILES + t, :], in_=row_major[:])

@@ -32,9 +32,9 @@ NORM_FLOOR = 1e-12
 BN_EPS = 1e-5
 
 HALVES_AHEAD = 3
-SUM_LAG = 3
-NORM_STAGES = 4
-APPLY_LAG = BLOCKS + SUM_LAG + NORM_STAGES
+SUM_LAG = 2
+NORM_STAGES = 3
+APPLY_LAG = BLOCKS + SUM_LAG + GROUP_TILES - 1 + NORM_STAGES
 
 FLOPS = 2 * ROWS * K * CHANNELS
 
@@ -66,8 +66,8 @@ def tile_batchedgraphsagemean1_pb_kernel(
     with tc.tile_pool(name="keep", bufs=1) as keep, tc.tile_pool(name="work", bufs=2) as work, tc.manual_schedule():
         ident = keep.tile([P, P], F32)
         make_identity(nc, ident[:])
-        ones_col = keep.tile([P, 1], F32)
-        nc.vector.memset(ones_col[:], 1.0)
+        ones = keep.tile([P, P], F32)
+        nc.vector.memset(ones[:], 1.0)
 
         w_codes = keep.tile([P, STREAMS, STREAM_CHANNELS], U32, align_bytes=64)
         w_planes = keep.tile([P, STREAMS, STREAM_CHANNELS], U8, align_bytes=64)
@@ -84,7 +84,7 @@ def tile_batchedgraphsagemean1_pb_kernel(
             first_row += n_rows
 
         table_warm = keep.tile([P, 1], F32)
-        nc.scalar.activation(out=table_warm[:], in_=ones_col[:], func=ACT.Sqrt)
+        nc.scalar.activation(out=table_warm[:], in_=ones[:, 0:1], func=ACT.Abs_reciprocal_sqrt)
 
         x_raw = keep.tile([P, STREAMS, ROW_TILES, K], BF16)
 
@@ -121,9 +121,9 @@ def tile_batchedgraphsagemean1_pb_kernel(
         with tc.psum_pool(name="psum_front", bufs=1) as psum:
             grouped = {}
             operands = {}
-            squares = {}
-            square_sums = {}
-            chain = {}
+            stream_squares = {}
+            row_sums = {}
+            inv_norm = {}
             spread = {}
 
             def transpose_vectors():
@@ -172,43 +172,40 @@ def tile_batchedgraphsagemean1_pb_kernel(
                     stop=True,
                 )
                 nc.vector.tensor_scalar_add(out=h_all[:, g, c, :], in0=acc[:], scalar1=bias[:, c : c + 1])
-                squares[i] = work.tile([P, GROUP_ROWS], F32, name="squares", bufs=SUM_LAG + 2)
-                nc.scalar.activation(out=squares[i][:], in_=h_all[:, g, c, :], func=ACT.Square)
-
-            def sum_squares(i):
-                g, c = i // BLOCKS, i % BLOCKS
-                if c == 0:
-                    square_sums[g] = psum.tile([P, GROUP_TILES, BLOCKS], F32, name="square_sums", bufs=1)
-                for t in range(GROUP_TILES):
-                    nc.tensor.matmul(
-                        out=square_sums[g][:, t, c : c + 1],
-                        lhsT=squares[i][:, t * P : (t + 1) * P],
-                        rhs=ones_col[:],
-                        start=True,
-                        stop=True,
+                m = g * STREAMS + s
+                if c % STREAM_BLOCKS == 0:
+                    stream_squares[m] = work.tile([P, GROUP_ROWS], F32, name="stream_squares", bufs=3)
+                    nc.scalar.activation(out=stream_squares[m][:], in_=h_all[:, g, c, :], func=ACT.Square)
+                else:
+                    squares = work.tile([P, GROUP_ROWS], F32, tag="squares", bufs=4)
+                    nc.scalar.activation(out=squares[:], in_=h_all[:, g, c, :], func=ACT.Square)
+                    nc.gpsimd.tensor_tensor(
+                        out=stream_squares[m][:], in0=stream_squares[m][:], in1=squares[:], op=ALU.add
                     )
+
+            def sum_squares(m, t):
+                g, s = m // STREAMS, m % STREAMS
+                if s == 0 and t == 0:
+                    row_sums[g] = psum.tile([P, GROUP_ROWS], F32, name="row_sums", bufs=1)
+                nc.tensor.matmul(
+                    out=row_sums[g][:, t * P : (t + 1) * P],
+                    lhsT=ones[:],
+                    rhs=stream_squares[m][:, t * P : (t + 1) * P],
+                    start=(s == 0 and t == 0),
+                    stop=(s == STREAMS - 1 and t == GROUP_TILES - 1),
+                )
 
             def norm_stage(g, stage):
                 if stage == 0:
-                    chain[g] = [work.tile([P, GROUP_TILES], F32, name="chain%d" % n) for n in range(4)]
-                total, floored, norm, inv_norm = chain[g]
-                if stage == 0:
-                    nc.vector.tensor_reduce(out=total[:], in_=square_sums[g][:], axis=AXIS.X, op=ALU.add)
-                    nc.vector.tensor_scalar_max(out=floored[:], in0=total[:], scalar1=NORM_FLOOR * NORM_FLOOR)
+                    inv_norm[g] = work.tile([P, GROUP_ROWS], F32, name="inv_norm")
+                    nc.vector.tensor_scalar_max(
+                        out=inv_norm[g][:], in0=row_sums[g][:], scalar1=NORM_FLOOR * NORM_FLOOR
+                    )
                 if stage == 1:
-                    nc.scalar.activation(out=norm[:], in_=floored[:], func=ACT.Sqrt)
+                    nc.scalar.activation(out=inv_norm[g][:], in_=inv_norm[g][:], func=ACT.Abs_reciprocal_sqrt)
                 if stage == 2:
-                    nc.vector.reciprocal(out=inv_norm[:], in_=norm[:])
-                if stage == 3:
                     spread[g] = psum.tile([P, GROUP_ROWS], F32, name="spread", bufs=2)
-                    for t in range(GROUP_TILES):
-                        nc.tensor.matmul(
-                            out=spread[g][:, t * P : (t + 1) * P],
-                            lhsT=inv_norm[:, t : t + 1].to_broadcast([P, P]),
-                            rhs=ident[:],
-                            start=True,
-                            stop=True,
-                        )
+                    nc.tensor.matmul(out=spread[g][:], lhsT=ident[:], rhs=inv_norm[g][:], start=True, stop=True)
 
             def normalise(i):
                 g, c = i // BLOCKS, i % BLOCKS
@@ -233,7 +230,7 @@ def tile_batchedgraphsagemean1_pb_kernel(
                     quantise(q // 2)
 
             for step in range(TILES + APPLY_LAG):
-                g, stage = divmod(step - BLOCKS - SUM_LAG, BLOCKS)
+                g, stage = divmod(step - APPLY_LAG + NORM_STAGES, BLOCKS)
                 if 0 <= g < GROUPS and stage < NORM_STAGES:
                     norm_stage(g, stage)
                 q = step // 2 + HALVES_AHEAD
@@ -243,8 +240,9 @@ def tile_batchedgraphsagemean1_pb_kernel(
                     quantise(q // 2)
                 if step < TILES:
                     project(step)
-                if 0 <= step - SUM_LAG < TILES:
-                    sum_squares(step - SUM_LAG)
+                summed = step - SUM_LAG - (STREAM_BLOCKS - 1)
+                if 0 <= summed < OPERANDS * GROUP_TILES:
+                    sum_squares(summed // GROUP_TILES, summed % GROUP_TILES)
                 if 0 <= step - APPLY_LAG:
                     normalise(step - APPLY_LAG)
 
@@ -252,7 +250,7 @@ def tile_batchedgraphsagemean1_pb_kernel(
             return keep.tile([P, BLOCKS], F32, name=name)
 
         total_r, total_rr, mean, mean_sq, second = small("total_r"), small("total_rr"), small("mean"), small("mean_sq"), small("second")
-        var_eps, std, inv_std, gain, mean_gain, shift = small("var_eps"), small("std"), small("inv_std"), small("gain"), small("mean_gain"), small("shift")
+        var_eps, inv_std, gain, mean_gain, shift = small("var_eps"), small("inv_std"), small("gain"), small("mean_gain"), small("shift")
         nc.vector.tensor_reduce(out=total_r[:], in_=sum_r[:], axis=AXIS.X, op=ALU.add)
         nc.vector.tensor_scalar_mul(out=mean[:], in0=total_r[:], scalar1=1.0 / ROWS)
         nc.vector.tensor_mul(out=mean_sq[:], in0=mean[:], in1=mean[:])
@@ -261,8 +259,7 @@ def tile_batchedgraphsagemean1_pb_kernel(
             out=second[:], in0=total_rr[:], scalar1=1.0 / ROWS, scalar2=BN_EPS, op0=ALU.mult, op1=ALU.add
         )
         nc.vector.tensor_sub(out=var_eps[:], in0=second[:], in1=mean_sq[:])
-        nc.scalar.activation(out=std[:], in_=var_eps[:], func=ACT.Sqrt)
-        nc.vector.reciprocal(out=inv_std[:], in_=std[:])
+        nc.scalar.activation(out=inv_std[:], in_=var_eps[:], func=ACT.Abs_reciprocal_sqrt)
         nc.vector.tensor_mul(out=gain[:], in0=gamma, in1=inv_std[:])
         nc.vector.tensor_mul(out=mean_gain[:], in0=mean[:], in1=gain[:])
         nc.vector.tensor_sub(out=shift[:], in0=beta, in1=mean_gain[:])

@@ -31,10 +31,15 @@ SCALE_ROWS = K // 32
 NORM_FLOOR = 1e-12
 BN_EPS = 1e-5
 
+BACK_STEPS = 2
 HALVES_AHEAD = 3
-SUM_LAG = 2
-NORM_STAGES = 3
-APPLY_LAG = BLOCKS + SUM_LAG + GROUP_TILES - 1 + NORM_STAGES
+QUANT_LAG = BACK_STEPS
+SUM_LAG = 3 * BACK_STEPS
+LAST_SUM = BLOCKS - 1 + SUM_LAG + GROUP_TILES - 1
+FLOOR_AT = LAST_SUM + 1
+RSQRT_AT = FLOOR_AT + 1
+SPREAD_AT = RSQRT_AT + 2 * BACK_STEPS
+APPLY_LAG = SPREAD_AT + 1
 
 FLOPS = 2 * ROWS * K * CHANNELS
 
@@ -174,7 +179,7 @@ def tile_batchedgraphsagemean1_pb_kernel(
                 nc.vector.tensor_scalar_add(out=h_all[:, g, c, :], in0=acc[:], scalar1=bias[:, c : c + 1])
                 m = g * STREAMS + s
                 if c % STREAM_BLOCKS == 0:
-                    stream_squares[m] = work.tile([P, GROUP_ROWS], F32, name="stream_squares", bufs=3)
+                    stream_squares[m] = work.tile([P, GROUP_ROWS], F32, name="stream_squares", bufs=4)
                     nc.scalar.activation(out=stream_squares[m][:], in_=h_all[:, g, c, :], func=ACT.Square)
                 else:
                     squares = work.tile([P, GROUP_ROWS], F32, tag="squares", bufs=4)
@@ -195,17 +200,16 @@ def tile_batchedgraphsagemean1_pb_kernel(
                     stop=(s == STREAMS - 1 and t == GROUP_TILES - 1),
                 )
 
-            def norm_stage(g, stage):
-                if stage == 0:
-                    inv_norm[g] = work.tile([P, GROUP_ROWS], F32, name="inv_norm")
-                    nc.vector.tensor_scalar_max(
-                        out=inv_norm[g][:], in0=row_sums[g][:], scalar1=NORM_FLOOR * NORM_FLOOR
-                    )
-                if stage == 1:
-                    nc.scalar.activation(out=inv_norm[g][:], in_=inv_norm[g][:], func=ACT.Abs_reciprocal_sqrt)
-                if stage == 2:
-                    spread[g] = psum.tile([P, GROUP_ROWS], F32, name="spread", bufs=2)
-                    nc.tensor.matmul(out=spread[g][:], lhsT=ident[:], rhs=inv_norm[g][:], start=True, stop=True)
+            def floor_sums(g):
+                inv_norm[g] = work.tile([P, GROUP_ROWS], F32, name="inv_norm")
+                nc.vector.tensor_scalar_max(out=inv_norm[g][:], in0=row_sums[g][:], scalar1=NORM_FLOOR * NORM_FLOOR)
+
+            def invert_norms(g):
+                nc.scalar.activation(out=inv_norm[g][:], in_=inv_norm[g][:], func=ACT.Abs_reciprocal_sqrt)
+
+            def spread_norms(g):
+                spread[g] = psum.tile([P, GROUP_ROWS], F32, name="spread", bufs=2)
+                nc.tensor.matmul(out=spread[g][:], lhsT=ident[:], rhs=inv_norm[g][:], start=True, stop=True)
 
             def normalise(i):
                 g, c = i // BLOCKS, i % BLOCKS
@@ -222,23 +226,23 @@ def tile_batchedgraphsagemean1_pb_kernel(
                 unread = work.tile([P, GROUP_ROWS], F32, tag="unread", bufs=3)
                 nc.scalar.activation(out=unread[:], in_=r, func=ACT.Square, accum_out=sum_rr[:, c, g : g + 1])
 
-            transpose_half(0)
-            transpose_vectors()
-            for q in range(1, HALVES_AHEAD):
-                transpose_half(q)
-                if q % 2 == 1:
-                    quantise(q // 2)
-
-            for step in range(TILES + APPLY_LAG):
-                g, stage = divmod(step - APPLY_LAG + NORM_STAGES, BLOCKS)
-                if 0 <= g < GROUPS and stage < NORM_STAGES:
-                    norm_stage(g, stage)
-                q = step // 2 + HALVES_AHEAD
-                if q < HALVES and step % 2 == 0:
+            for step in range(-2 * HALVES_AHEAD, TILES + APPLY_LAG):
+                if step == -1:
+                    transpose_vectors()
+                for g in range(GROUPS):
+                    if step == g * BLOCKS + FLOOR_AT:
+                        floor_sums(g)
+                    if step == g * BLOCKS + RSQRT_AT:
+                        invert_norms(g)
+                    if step == g * BLOCKS + SPREAD_AT:
+                        spread_norms(g)
+                q, odd_step = divmod(step + 2 * HALVES_AHEAD, 2)
+                if q < HALVES and not odd_step:
                     transpose_half(q)
-                if q < HALVES and step % 2 == 1 and q % 2 == 1:
+                q, odd_step = divmod(step + 2 * HALVES_AHEAD - QUANT_LAG, 2)
+                if 0 <= q < HALVES and not odd_step and q % 2 == 1:
                     quantise(q // 2)
-                if step < TILES:
+                if 0 <= step < TILES:
                     project(step)
                 summed = step - SUM_LAG - (STREAM_BLOCKS - 1)
                 if 0 <= summed < OPERANDS * GROUP_TILES:

@@ -31,8 +31,8 @@ SCALE_ROWS = K // 32
 NORM_FLOOR = 1e-12
 BN_EPS = 1e-5
 
-BACK_STEPS = 2
-HALVES_AHEAD = 3
+BACK_STEPS = 3
+HALVES_AHEAD = 4
 QUANT_LAG = BACK_STEPS
 SUM_LAG = 3 * BACK_STEPS
 LAST_SUM = BLOCKS - 1 + SUM_LAG + GROUP_TILES - 1
@@ -179,7 +179,7 @@ def tile_batchedgraphsagemean1_pb_kernel(
                 nc.vector.tensor_scalar_add(out=h_all[:, g, c, :], in0=acc[:], scalar1=bias[:, c : c + 1])
                 m = g * STREAMS + s
                 if c % STREAM_BLOCKS == 0:
-                    stream_squares[m] = work.tile([P, GROUP_ROWS], F32, name="stream_squares", bufs=4)
+                    stream_squares[m] = work.tile([P, GROUP_ROWS], F32, name="stream_squares", bufs=5)
                     nc.scalar.activation(out=stream_squares[m][:], in_=h_all[:, g, c, :], func=ACT.Square)
                 else:
                     squares = work.tile([P, GROUP_ROWS], F32, tag="squares", bufs=4)

@@ -34,8 +34,8 @@ BN_EPS = 1e-5
 BACK_STEPS = 3
 HALVES_AHEAD = 4
 QUANT_LAG = BACK_STEPS
-SUM_LAG = 3 * BACK_STEPS
-LAST_SUM = BLOCKS - 1 + SUM_LAG + GROUP_TILES - 1
+SUM_LAG = 2 * BACK_STEPS
+LAST_SUM = BLOCKS - 1 + SUM_LAG
 FLOOR_AT = LAST_SUM + 1
 RSQRT_AT = FLOOR_AT + 1
 SPREAD_AT = RSQRT_AT + 2 * BACK_STEPS
@@ -71,7 +71,7 @@ def tile_batchedgraphsagemean1_pb_kernel(
     with tc.tile_pool(name="keep", bufs=1) as keep, tc.tile_pool(name="work", bufs=2) as work, tc.manual_schedule():
         ident = keep.tile([P, P], F32)
         make_identity(nc, ident[:])
-        ones = keep.tile([P, P], F32)
+        ones = keep.tile([P, 1], F32)
         nc.vector.memset(ones[:], 1.0)
 
         w_codes = keep.tile([P, STREAMS, STREAM_CHANNELS], U32, align_bytes=64)
@@ -126,7 +126,7 @@ def tile_batchedgraphsagemean1_pb_kernel(
         with tc.psum_pool(name="psum_front", bufs=1) as psum:
             grouped = {}
             operands = {}
-            stream_squares = {}
+            squares = {}
             row_sums = {}
             inv_norm = {}
             spread = {}
@@ -177,39 +177,38 @@ def tile_batchedgraphsagemean1_pb_kernel(
                     stop=True,
                 )
                 nc.vector.tensor_scalar_add(out=h_all[:, g, c, :], in0=acc[:], scalar1=bias[:, c : c + 1])
-                m = g * STREAMS + s
-                if c % STREAM_BLOCKS == 0:
-                    stream_squares[m] = work.tile([P, GROUP_ROWS], F32, name="stream_squares", bufs=5)
-                    nc.scalar.activation(out=stream_squares[m][:], in_=h_all[:, g, c, :], func=ACT.Square)
-                else:
-                    squares = work.tile([P, GROUP_ROWS], F32, tag="squares", bufs=4)
-                    nc.scalar.activation(out=squares[:], in_=h_all[:, g, c, :], func=ACT.Square)
-                    nc.gpsimd.tensor_tensor(
-                        out=stream_squares[m][:], in0=stream_squares[m][:], in1=squares[:], op=ALU.add
+                squares[i] = work.tile([P, GROUP_ROWS], F32, name="squares", bufs=SUM_LAG + 2)
+                nc.scalar.activation(out=squares[i][:], in_=h_all[:, g, c, :], func=ACT.Square)
+
+            def sum_squares(i):
+                g, c = i // BLOCKS, i % BLOCKS
+                if c == 0:
+                    row_sums[g] = psum.tile([P, GROUP_TILES, P], F32, name="row_sums", bufs=1)
+                for t in range(GROUP_TILES):
+                    nc.tensor.matmul(
+                        out=row_sums[g][:, t, :],
+                        lhsT=squares[i][:, t * P : (t + 1) * P],
+                        rhs=ident[:],
+                        is_transpose=True,
+                        start=(c == 0 and t == 0),
+                        stop=(c == BLOCKS - 1 and t == GROUP_TILES - 1),
                     )
 
-            def sum_squares(m, t):
-                g, s = m // STREAMS, m % STREAMS
-                if s == 0 and t == 0:
-                    row_sums[g] = psum.tile([P, GROUP_ROWS], F32, name="row_sums", bufs=1)
-                nc.tensor.matmul(
-                    out=row_sums[g][:, t * P : (t + 1) * P],
-                    lhsT=ones[:],
-                    rhs=stream_squares[m][:, t * P : (t + 1) * P],
-                    start=(s == 0 and t == 0),
-                    stop=(s == STREAMS - 1 and t == GROUP_TILES - 1),
-                )
-
             def floor_sums(g):
-                inv_norm[g] = work.tile([P, GROUP_ROWS], F32, name="inv_norm")
-                nc.vector.tensor_scalar_max(out=inv_norm[g][:], in0=row_sums[g][:], scalar1=NORM_FLOOR * NORM_FLOOR)
+                norm_sq = work.tile([P, GROUP_TILES], F32, name="norm_sq")
+                nc.vector.tensor_reduce(out=norm_sq[:], in_=row_sums[g][:], axis=AXIS.X, op=ALU.add)
+                inv_norm[g] = work.tile([P, GROUP_TILES], F32, name="inv_norm")
+                nc.vector.tensor_scalar_max(out=inv_norm[g][:], in0=norm_sq[:], scalar1=NORM_FLOOR * NORM_FLOOR)
 
             def invert_norms(g):
                 nc.scalar.activation(out=inv_norm[g][:], in_=inv_norm[g][:], func=ACT.Abs_reciprocal_sqrt)
 
             def spread_norms(g):
                 spread[g] = psum.tile([P, GROUP_ROWS], F32, name="spread", bufs=2)
-                nc.tensor.matmul(out=spread[g][:], lhsT=ident[:], rhs=inv_norm[g][:], start=True, stop=True)
+                for t in range(GROUP_TILES):
+                    nc.tensor.transpose(
+                        spread[g][:, t * P : (t + 1) * P], inv_norm[g][:, t : t + 1].to_broadcast([P, P]), ident[:]
+                    )
 
             def normalise(i):
                 g, c = i // BLOCKS, i % BLOCKS
@@ -244,9 +243,8 @@ def tile_batchedgraphsagemean1_pb_kernel(
                     quantise(q // 2)
                 if 0 <= step < TILES:
                     project(step)
-                summed = step - SUM_LAG - (STREAM_BLOCKS - 1)
-                if 0 <= summed < OPERANDS * GROUP_TILES:
-                    sum_squares(summed // GROUP_TILES, summed % GROUP_TILES)
+                if 0 <= step - SUM_LAG < TILES:
+                    sum_squares(step - SUM_LAG)
                 if 0 <= step - APPLY_LAG:
                     normalise(step - APPLY_LAG)
 

@@ -41,6 +41,9 @@ RSQRT_AT = FLOOR_AT + 1
 SPREAD_AT = RSQRT_AT + 2 * BACK_STEPS
 APPLY_LAG = SPREAD_AT + 1
 
+SCALAR_EMPTIES = (1, 4, 6, 9, 11)
+SCALAR_SQUARES = (3, 7, 10)
+
 FLOPS = 2 * ROWS * K * CHANNELS
 
 
@@ -176,9 +179,16 @@ def tile_batchedgraphsagemean1_pb_kernel(
                     start=True,
                     stop=True,
                 )
-                nc.vector.tensor_scalar_add(out=h_all[:, g, c, :], in0=acc[:], scalar1=bias[:, c : c + 1])
+                h = h_all[:, g, c, :]
+                if c in SCALAR_EMPTIES:
+                    nc.scalar.activation(out=h, in_=acc[:], func=ACT.Identity, bias=bias[:, c : c + 1])
+                else:
+                    nc.vector.tensor_scalar_add(out=h, in0=acc[:], scalar1=bias[:, c : c + 1])
                 squares[i] = work.tile([P, GROUP_ROWS], F32, name="squares", bufs=SUM_LAG + 2)
-                nc.scalar.activation(out=squares[i][:], in_=h_all[:, g, c, :], func=ACT.Square)
+                if c in SCALAR_SQUARES:
+                    nc.scalar.activation(out=squares[i][:], in_=h, func=ACT.Square)
+                else:
+                    nc.gpsimd.tensor_tensor(out=squares[i][:], in0=h, in1=h, op=ALU.mult)
 
             def sum_squares(i):
                 g, c = i // BLOCKS, i % BLOCKS
@@ -222,7 +232,7 @@ def tile_batchedgraphsagemean1_pb_kernel(
                     op1=ALU.mult,
                     accum_out=sum_r[:, c, g : g + 1],
                 )
-                unread = work.tile([P, GROUP_ROWS], F32, tag="unread", bufs=3)
+                unread = work.tile([P, GROUP_ROWS], F32, tag="unread", bufs=2)
                 nc.scalar.activation(out=unread[:], in_=r, func=ACT.Square, accum_out=sum_rr[:, c, g : g + 1])
 
             for step in range(-2 * HALVES_AHEAD, TILES + APPLY_LAG):

@@ -71,7 +71,7 @@ def tile_batchedgraphsagemean1_pb_kernel(
     weight_scales = [Wx_w_scales, Wn_w_scales, Wr_w_scales]
     out_rows = out.flatten_outer_dims().rearrange("(p n) c -> p n c", n=ROW_TILES)
 
-    with tc.tile_pool(name="keep", bufs=1) as keep, tc.tile_pool(name="work", bufs=2) as work, tc.manual_schedule():
+    with tc.tile_pool(name="keep", bufs=1) as keep, tc.tile_pool(name="work", bufs=2) as work:
         ident = keep.tile([P, P], F32)
         make_identity(nc, ident[:])
         ones = keep.tile([P, 1], F32)

@@ -44,6 +44,9 @@ APPLY_LAG = SPREAD_AT + 1
 SCALAR_EMPTIES = (1, 4, 6, 9, 11)
 SCALAR_SQUARES = (3, 7, 10)
 
+YT_BANKS = (("acc", 3), ("xt", 2), ("acc", 3), ("xt", 2), ("acc", 3), ("row_sums", 1))
+ITEMS_A_STEP = 3
+
 FLOPS = 2 * ROWS * K * CHANNELS
 
 
@@ -126,7 +129,13 @@ def tile_batchedgraphsagemean1_pb_kernel(
         gamma = vec_cols[:, BLOCKS : 2 * BLOCKS]
         beta = vec_cols[:, 2 * BLOCKS : 3 * BLOCKS]
 
-        with tc.psum_pool(name="psum_front", bufs=1) as psum:
+        def small(name):
+            return keep.tile([P, BLOCKS], F32, name=name)
+
+        total_r, total_rr, mean, mean_sq, second = small("total_r"), small("total_rr"), small("mean"), small("mean_sq"), small("second")
+        var_eps, inv_std, gain, mean_gain, shift = small("var_eps"), small("inv_std"), small("gain"), small("mean_gain"), small("shift")
+
+        with tc.psum_pool(name="psum", bufs=1) as psum:
             grouped = {}
             operands = {}
             squares = {}
@@ -193,7 +202,8 @@ def tile_batchedgraphsagemean1_pb_kernel(
             def sum_squares(i):
                 g, c = i // BLOCKS, i % BLOCKS
                 if c == 0:
-                    row_sums[g] = psum.tile([P, GROUP_TILES, P], F32, name="row_sums", bufs=1)
+                    sums = psum.tile([P, GROUP_TILES, P], F32, tag="row_sums", bufs=1)
+                    row_sums[g] = sums
                 for t in range(GROUP_TILES):
                     nc.tensor.matmul(
                         out=row_sums[g][:, t, :],
@@ -235,6 +245,68 @@ def tile_batchedgraphsagemean1_pb_kernel(
                 unread = work.tile([P, GROUP_ROWS], F32, tag="unread", bufs=2)
                 nc.scalar.activation(out=unread[:], in_=r, func=ACT.Square, accum_out=sum_rr[:, c, g : g + 1])
 
+            def statistics(s):
+                cs = slice(s * STREAM_BLOCKS, (s + 1) * STREAM_BLOCKS)
+                nc.vector.tensor_reduce(out=total_r[:, cs], in_=sum_r[:, cs, :], axis=AXIS.X, op=ALU.add)
+                nc.vector.tensor_scalar_mul(out=mean[:, cs], in0=total_r[:, cs], scalar1=1.0 / ROWS)
+                nc.vector.tensor_mul(out=mean_sq[:, cs], in0=mean[:, cs], in1=mean[:, cs])
+                nc.vector.tensor_reduce(out=total_rr[:, cs], in_=sum_rr[:, cs, :], axis=AXIS.X, op=ALU.add)
+                nc.vector.tensor_scalar(
+                    out=second[:, cs], in0=total_rr[:, cs], scalar1=1.0 / ROWS, scalar2=BN_EPS, op0=ALU.mult, op1=ALU.add
+                )
+                nc.vector.tensor_sub(out=var_eps[:, cs], in0=second[:, cs], in1=mean_sq[:, cs])
+                nc.scalar.activation(out=inv_std[:, cs], in_=var_eps[:, cs], func=ACT.Abs_reciprocal_sqrt)
+                nc.vector.tensor_mul(out=gain[:, cs], in0=gamma[:, cs], in1=inv_std[:, cs])
+                nc.vector.tensor_mul(out=mean_gain[:, cs], in0=mean[:, cs], in1=gain[:, cs])
+                nc.vector.tensor_sub(out=shift[:, cs], in0=beta[:, cs], in1=mean_gain[:, cs])
+
+            def scale_and_shift(g, c):
+                y = h_all[:, g, c, :]
+                engine = c % 3
+                if engine == 0:
+                    nc.vector.tensor_scalar(
+                        out=y, in0=y, scalar1=gain[:, c : c + 1], scalar2=shift[:, c : c + 1], op0=ALU.mult, op1=ALU.add
+                    )
+                elif engine == 1:
+                    nc.scalar.activation(out=y, in_=y, func=ACT.Identity, scale=gain[:, c : c + 1], bias=shift[:, c : c + 1])
+                else:
+                    nc.gpsimd.tensor_scalar(
+                        out=y, in0=y, scalar1=gain[:, c : c + 1], scalar2=shift[:, c : c + 1], op0=ALU.mult, op1=ALU.add
+                    )
+
+            def store_tile(s, g, t):
+                number = (s * GROUPS + g) * GROUP_TILES + t
+                if t % 2 == 0:
+                    rows_out = work.tile([P, 2, STREAM_CHANNELS], F32, tag="staged", bufs=6)
+                    staged[s, g, t // 2] = rows_out
+                tag, bufs = YT_BANKS[number % len(YT_BANKS)]
+                yt = psum.tile([P, STREAM_CHANNELS], F32, tag=tag, bufs=bufs)
+                for j in range(STREAM_BLOCKS):
+                    nc.tensor.transpose(
+                        yt[:, j * P : (j + 1) * P], h_all[:, g, s * STREAM_BLOCKS + j, t * P : (t + 1) * P], ident[:]
+                    )
+                landing = staged[s, g, t // 2][:, t % 2, :]
+                if number % 2 == 0:
+                    nc.vector.tensor_copy(out=landing, in_=yt[:])
+                else:
+                    nc.scalar.copy(out=landing, in_=yt[:])
+                if t % 2 == 1:
+                    row0 = g * GROUP_TILES + t - 1
+                    nc.sync.dma_start(
+                        out=out_rows[:, row0 : row0 + 2, s * STREAM_CHANNELS : (s + 1) * STREAM_CHANNELS], in_=staged[s, g, t // 2][:]
+                    )
+
+            def finish_items(s):
+                items = [(scale_and_shift, 0, s * STREAM_BLOCKS + j) for j in range(STREAM_BLOCKS)]
+                for g in range(GROUPS):
+                    for t in range(GROUP_TILES):
+                        if g + 1 < GROUPS:
+                            items.append((scale_and_shift, g + 1, s * STREAM_BLOCKS + t))
+                        items.append((store_tile, s, g, t))
+                return items
+
+            staged = {}
+            waiting = []
             for step in range(-2 * HALVES_AHEAD, TILES + APPLY_LAG):
                 if step == -1:
                     transpose_vectors()
@@ -257,51 +329,13 @@ def tile_batchedgraphsagemean1_pb_kernel(
                     sum_squares(step - SUM_LAG)
                 if 0 <= step - APPLY_LAG:
                     normalise(step - APPLY_LAG)
-
-        def small(name):
-            return keep.tile([P, BLOCKS], F32, name=name)
-
-        total_r, total_rr, mean, mean_sq, second = small("total_r"), small("total_rr"), small("mean"), small("mean_sq"), small("second")
-        var_eps, inv_std, gain, mean_gain, shift = small("var_eps"), small("inv_std"), small("gain"), small("mean_gain"), small("shift")
-        nc.vector.tensor_reduce(out=total_r[:], in_=sum_r[:], axis=AXIS.X, op=ALU.add)
-        nc.vector.tensor_scalar_mul(out=mean[:], in0=total_r[:], scalar1=1.0 / ROWS)
-        nc.vector.tensor_mul(out=mean_sq[:], in0=mean[:], in1=mean[:])
-        nc.vector.tensor_reduce(out=total_rr[:], in_=sum_rr[:], axis=AXIS.X, op=ALU.add)
-        nc.vector.tensor_scalar(
-            out=second[:], in0=total_rr[:], scalar1=1.0 / ROWS, scalar2=BN_EPS, op0=ALU.mult, op1=ALU.add
-        )
-        nc.vector.tensor_sub(out=var_eps[:], in0=second[:], in1=mean_sq[:])
-        nc.scalar.activation(out=inv_std[:], in_=var_eps[:], func=ACT.Abs_reciprocal_sqrt)
-        nc.vector.tensor_mul(out=gain[:], in0=gamma, in1=inv_std[:])
-        nc.vector.tensor_mul(out=mean_gain[:], in0=mean[:], in1=gain[:])
-        nc.vector.tensor_sub(out=shift[:], in0=beta, in1=mean_gain[:])
-
-        def scale_and_shift(g, c):
-            y = h_all[:, g, c, :]
-            nc.vector.tensor_scalar(
-                out=y, in0=y, scalar1=gain[:, c : c + 1], scalar2=shift[:, c : c + 1], op0=ALU.mult, op1=ALU.add
-            )
-
-        with tc.psum_pool(name="psum_back", bufs=6) as psum:
-            for c in range(BLOCKS):
-                scale_and_shift(0, c)
-            for g in range(GROUPS):
-                for t in range(GROUP_TILES):
-                    if g + 1 < GROUPS:
-                        for c in range(t * BLOCKS // GROUP_TILES, (t + 1) * BLOCKS // GROUP_TILES):
-                            scale_and_shift(g + 1, c)
-                    row_major = work.tile([P, CHANNELS], F32, tag="row_major", bufs=4)
-                    for s in range(STREAMS):
-                        yt = psum.tile([P, STREAM_CHANNELS], F32, tag="yt")
-                        for j in range(STREAM_BLOCKS):
-                            nc.tensor.transpose(
-                                yt[:, j * P : (j + 1) * P],
-                                h_all[:, g, s * STREAM_BLOCKS + j, t * P : (t + 1) * P],
-                                ident[:],
-                            )
-                        landing = row_major[:, s * STREAM_CHANNELS : (s + 1) * STREAM_CHANNELS]
-                        if s == 0:
-                            nc.vector.tensor_copy(out=landing, in_=yt[:])
-                        else:
-                            nc.scalar.copy(out=landing, in_=yt[:])
-                    nc.sync.dma_start(out=out_rows[:, g * GROUP_TILES + t, :], in_=row_major[:])
+                    done_tiles = step - APPLY_LAG - (TILES - BLOCKS) + 1
+                    if done_tiles > 0 and done_tiles % STREAM_BLOCKS == 0:
+                        s = done_tiles // STREAM_BLOCKS - 1
+                        statistics(s)
+                        waiting.extend(finish_items(s))
+                    for item in waiting[:ITEMS_A_STEP]:
+                        item[0](*item[1:])
+                    waiting[:ITEMS_A_STEP] = []
+            for item in waiting:
+                item[0](*item[1:])

@@ -33,12 +33,13 @@ BN_EPS = 1e-5
 
 BACK_STEPS = 3
 HALVES_AHEAD = 4
+FIRST_HALVES = 2 * STREAMS
 QUANT_LAG = BACK_STEPS
-SUM_LAG = 2 * BACK_STEPS
+SUM_LAG = 10
 LAST_SUM = BLOCKS - 1 + SUM_LAG
 FLOOR_AT = LAST_SUM + 1
 RSQRT_AT = FLOOR_AT + 1
-SPREAD_AT = RSQRT_AT + 2 * BACK_STEPS
+SPREAD_AT = RSQRT_AT + 2
 APPLY_LAG = SPREAD_AT + 1
 
 SCALAR_EMPTIES = (1, 4, 6, 9, 11)
@@ -46,6 +47,9 @@ SCALAR_SQUARES = (3, 7, 10)
 
 YT_BANKS = (("acc", 3), ("xt", 2), ("acc", 3), ("xt", 2), ("acc", 3), ("row_sums", 1))
 ITEMS_A_STEP = 3
+
+SLOT_WORDS = 2 * 2 * STREAM_CHANNELS
+STAGING_SLOTS = STREAMS * ROW_TILES * K // SLOT_WORDS
 
 FLOPS = 2 * ROWS * K * CHANNELS
 
@@ -121,6 +125,8 @@ def tile_batchedgraphsagemean1_pb_kernel(
         for q in range(2 * STREAMS, HALVES):
             load_half(q)
 
+        staging = x_raw[:].rearrange("p s n k -> p (s n k)")
+
         h_all = keep.tile([P, GROUPS, BLOCKS, GROUP_ROWS], F32)
         sum_r = keep.tile([P, BLOCKS, GROUPS], F32)
         sum_rr = keep.tile([P, BLOCKS, GROUPS], F32)
@@ -154,7 +160,7 @@ def tile_batchedgraphsagemean1_pb_kernel(
                 m, half = q // 2, q % 2
                 g, s = m // STREAMS, m % STREAMS
                 if half == 0:
-                    grouped[m] = work.tile([P, GROUP_ROWS, 2], F32, name="grouped", bufs=3, align_bytes=64)
+                    grouped[m] = work.tile([P, GROUP_ROWS, 2], F32, name="grouped", bufs=5, align_bytes=64)
                 xt = psum.tile([P, 2, HALF_TILES * P], F32, tag="xt", bufs=2)
                 for i in range(HALF_TILES):
                     words = x_raw[:, s, g * GROUP_TILES + half * HALF_TILES + i, :].bitcast(F32)
@@ -164,8 +170,8 @@ def tile_batchedgraphsagemean1_pb_kernel(
                 nc.scalar.copy(out=grouped[m][:, rows, :], in_=xt[:].rearrange("p u r -> p r u"))
 
             def quantise(m):
-                codes = work.tile([P, GROUP_ROWS], U32, tag="codes", bufs=2 * STREAMS, align_bytes=64)
-                plane = work.tile([P, GROUP_ROWS], U8, tag="plane", bufs=2 * STREAMS, align_bytes=64)
+                codes = work.tile([P, GROUP_ROWS], U32, tag="codes", bufs=OPERANDS, align_bytes=64)
+                plane = work.tile([P, GROUP_ROWS], U8, tag="plane", bufs=OPERANDS, align_bytes=64)
                 nc.vector.quantize_mx(
                     out=codes[:].bitcast(FP8X4),
                     scales=plane[:],
@@ -277,8 +283,8 @@ def tile_batchedgraphsagemean1_pb_kernel(
             def store_tile(s, g, t):
                 number = (s * GROUPS + g) * GROUP_TILES + t
                 if t % 2 == 0:
-                    rows_out = work.tile([P, 2, STREAM_CHANNELS], F32, tag="staged", bufs=6)
-                    staged[s, g, t // 2] = rows_out
+                    slot = number // 2 % STAGING_SLOTS
+                    staged[s, g, t // 2] = staging[:, slot * SLOT_WORDS : (slot + 1) * SLOT_WORDS].bitcast(F32).rearrange("p (t c) -> p t c", t=2)
                 tag, bufs = YT_BANKS[number % len(YT_BANKS)]
                 yt = psum.tile([P, STREAM_CHANNELS], F32, tag=tag, bufs=bufs)
                 for j in range(STREAM_BLOCKS):
@@ -293,7 +299,7 @@ def tile_batchedgraphsagemean1_pb_kernel(
                 if t % 2 == 1:
                     row0 = g * GROUP_TILES + t - 1
                     nc.sync.dma_start(
-                        out=out_rows[:, row0 : row0 + 2, s * STREAM_CHANNELS : (s + 1) * STREAM_CHANNELS], in_=staged[s, g, t // 2][:]
+                        out=out_rows[:, row0 : row0 + 2, s * STREAM_CHANNELS : (s + 1) * STREAM_CHANNELS], in_=staged[s, g, t // 2]
                     )
 
             def finish_items(s):
@@ -305,6 +311,9 @@ def tile_batchedgraphsagemean1_pb_kernel(
                         items.append((store_tile, s, g, t))
                 return items
 
+            half_at = {}
+            for q in range(HALVES):
+                half_at[2 * (min(q, FIRST_HALVES) - HALVES_AHEAD) + max(q - FIRST_HALVES, 0)] = q
             staged = {}
             waiting = []
             for step in range(-2 * HALVES_AHEAD, TILES + APPLY_LAG):
@@ -317,11 +326,10 @@ def tile_batchedgraphsagemean1_pb_kernel(
                         invert_norms(g)
                     if step == g * BLOCKS + SPREAD_AT:
                         spread_norms(g)
-                q, odd_step = divmod(step + 2 * HALVES_AHEAD, 2)
-                if q < HALVES and not odd_step:
-                    transpose_half(q)
-                q, odd_step = divmod(step + 2 * HALVES_AHEAD - QUANT_LAG, 2)
-                if 0 <= q < HALVES and not odd_step and q % 2 == 1:
+                if step in half_at:
+                    transpose_half(half_at[step])
+                q = half_at.get(step - QUANT_LAG, 0)
+                if q % 2 == 1:
                     quantise(q // 2)
                 if 0 <= step < TILES:
                     project(step)

@@ -23,54 +23,47 @@ ROW_TILES = ROWS // P
 GROUP_TILES = 4
 GROUP_ROWS = GROUP_TILES * P
 GROUPS = ROW_TILES // GROUP_TILES
-TILES = GROUPS * BLOCKS
+STEPS = GROUPS * BLOCKS
 OPERANDS = GROUPS * STREAMS
-HALF_TILES = GROUP_TILES // 2
-HALVES = 2 * OPERANDS
+HALF_TILES = 2
+HALVES = [(g, s, t) for g in range(GROUPS) for s in range(STREAMS) for t in range(0, GROUP_TILES, HALF_TILES)]
 SCALE_ROWS = K // 32
 NORM_FLOOR = 1e-12
 BN_EPS = 1e-5
 
-BACK_STEPS = 3
-HALVES_AHEAD = 4
-FIRST_HALVES = 2 * STREAMS
-QUANT_LAG = BACK_STEPS
-SUM_LAG = 10
-LAST_SUM = BLOCKS - 1 + SUM_LAG
-FLOOR_AT = LAST_SUM + 1
-RSQRT_AT = FLOOR_AT + 1
-SPREAD_AT = RSQRT_AT + 2
-APPLY_LAG = SPREAD_AT + 1
+RUN = 2
+HALVES_AHEAD = 8 / 2
+COPY_LAG = 1.5
+QUANT_LAG = 3
+EMPTY_LAG = 0.4
+SQUARE_LAG = 1.6
+FIRST_SUM_LAG = 7
+SUM_LAG = 9
+LAST_SUM_LAG = 3
+CHAIN_LAG = 0.7
+APPLY_LAG = 1
+SQUARE_R_LAG = 1
+STAT_LAG = 0.5
+STORE_PACE = 0.4
+LAND_LAG = 1
+FAST = 0.6
+DEFER_FROM = (GROUPS, 3, 2)
+DEFER_LAG = (0, 1, 0.5)
+DEFER_PACE = (0, 1, 1.8)
+OUT_LAG = 0.3
 
-SCALAR_EMPTIES = (1, 4, 6, 9, 11)
-SCALAR_SQUARES = (3, 7, 10)
-
-YT_BANKS = (("acc", 3), ("xt", 2), ("acc", 3), ("xt", 2), ("acc", 3), ("row_sums", 1))
-ITEMS_A_STEP = 3
-
-SLOT_WORDS = 2 * 2 * STREAM_CHANNELS
-STAGING_SLOTS = STREAMS * ROW_TILES * K // SLOT_WORDS
+SCALAR_EMPTIES = ((1, 4, 6, 9, 11), (1, 4, 6, 9, 11), (1, 4, 6, 9, 11), (1, 4, 6, 9, 11))
+SCALAR_SQUARES = ((1,4,6,9,11), (0,3,6,9), (3, 7, 10), (3,10))
+YT_BANKS = (("acc", 3), ("spread", 2), ("acc", 3), ("spread", 2), ("acc", 3), ("row_sums", 1))
+STAGING_SLOTS = 12
+STORED_ALONE = (0, 1)
+SLOT_WORDS = 2048
 
 FLOPS = 2 * ROWS * K * CHANNELS
 
 
 def tile_batchedgraphsagemean1_pb_kernel(
-    tc,
-    x,
-    nb,
-    mu,
-    Wx_w_words,
-    Wx_w_scales,
-    Wx_b,
-    Wn_w_words,
-    Wn_w_scales,
-    Wn_b,
-    Wr_w_words,
-    Wr_w_scales,
-    Wr_b,
-    bn_gamma,
-    bn_beta,
-    out,
+    tc, x, nb, mu, Wx_w_words, Wx_w_scales, Wx_b, Wn_w_words, Wn_w_scales, Wn_b, Wr_w_words, Wr_w_scales, Wr_b, bn_gamma, bn_beta, out
 ):
     nc = tc.nc
     streams = [src.flatten_outer_dims().rearrange("(p n) k -> p n k", n=ROW_TILES) for src in (x, nb, mu)]
@@ -83,57 +76,60 @@ def tile_batchedgraphsagemean1_pb_kernel(
         make_identity(nc, ident[:])
         ones = keep.tile([P, 1], F32)
         nc.vector.memset(ones[:], 1.0)
-
         w_codes = keep.tile([P, STREAMS, STREAM_CHANNELS], U32, align_bytes=64)
         w_planes = keep.tile([P, STREAMS, STREAM_CHANNELS], U8, align_bytes=64)
+        bias_rows = keep.tile([P, P], BF16)
+        nc.vector.memset(bias_rows[:], 0.0)
+        late_rows = keep.tile([P, P], BF16)
+        nc.vector.memset(late_rows[:], 0.0)
         nc.vector.memset(w_planes[:].bitcast(I32), 0)
 
-        vec_rows = keep.tile([P, P], BF16)
-        nc.vector.memset(vec_rows[:], 0.0)
-        first_row = 0
-        for vec in (Wx_b, Wn_b, Wr_b, bn_gamma, bn_beta):
-            n_rows = vec.shape[0] // P
-            nc.scalar.dma_start(
-                out=vec_rows[first_row : first_row + n_rows, :], in_=vec.rearrange("(r c) -> r c", c=P)
-            )
-            first_row += n_rows
+        def load_vectors(rows, vecs, queue):
+            first_row = 0
+            for vec in vecs:
+                n_rows = vec.shape[0] // P
+                queue.dma_start(out=rows[first_row : first_row + n_rows, :], in_=vec.rearrange("(r c) -> r c", c=P))
+                first_row += n_rows
 
+        load_vectors(bias_rows, (Wx_b, Wn_b, Wr_b), nc.scalar)
         table_warm = keep.tile([P, 1], F32)
         nc.scalar.activation(out=table_warm[:], in_=ones[:, 0:1], func=ACT.Abs_reciprocal_sqrt)
-
         x_raw = keep.tile([P, STREAMS, ROW_TILES, K], BF16)
 
-        def load_half(q):
-            g, s, half = q // (2 * STREAMS), q // 2 % STREAMS, q % 2
-            first = g * GROUP_TILES + half * HALF_TILES
+        def load_weight(s):
             nc.sync.dma_start(
-                out=x_raw[:, s, first : first + HALF_TILES, :], in_=streams[s][:, first : first + HALF_TILES, :]
+                out=w_codes[:, s, :].bitcast(I32), in_=weight_words[s][0].rearrange("p n t -> p (n t)").bitcast(I32)
             )
 
-        for s in range(STREAMS):
-            load_half(2 * s)
-            load_half(2 * s + 1)
-            nc.sync.dma_start(
-                out=w_codes[:, s, :].bitcast(I32),
-                in_=weight_words[s][0].rearrange("p n t -> p (n t)").bitcast(I32),
-            )
+        def load_planes(s):
             for quadrant in range(SCALE_ROWS // 4):
                 nc.sync.dma_start(
                     out=w_planes[32 * quadrant : 32 * quadrant + 4, s, :].bitcast(I32),
                     in_=weight_scales[s][0, 4 * quadrant : 4 * quadrant + 4, :].bitcast(I32),
                 )
-        for q in range(2 * STREAMS, HALVES):
-            load_half(q)
 
+        def load_rows(s, first, n):
+            rows = slice(first, first + n)
+            nc.sync.dma_start(out=x_raw[:, s, rows, :], in_=streams[s][:, rows, :])
+
+        for s in range(STREAMS):
+            load_rows(s, 0, 2)
+            load_rows(s, 2, 2)
+            load_weight(s)
+            load_planes(s)
+        for g in range(1, GROUPS):
+            for s in range(STREAMS):
+                for t in range(0, GROUP_TILES, HALF_TILES):
+                    load_rows(s, g * GROUP_TILES + t, HALF_TILES)
+        load_vectors(late_rows, (bn_gamma, bn_beta), nc.sync)
         staging = x_raw[:].rearrange("p s n k -> p (s n k)")
-
-        h_all = keep.tile([P, GROUPS, BLOCKS, GROUP_ROWS], F32)
+        h_all = keep.tile([P, BLOCKS, ROWS], F32)
         sum_r = keep.tile([P, BLOCKS, GROUPS], F32)
         sum_rr = keep.tile([P, BLOCKS, GROUPS], F32)
-        vec_cols = keep.tile([P, 3 * BLOCKS], F32)
-        bias = vec_cols[:, 0:BLOCKS]
-        gamma = vec_cols[:, BLOCKS : 2 * BLOCKS]
-        beta = vec_cols[:, 2 * BLOCKS : 3 * BLOCKS]
+        bias = keep.tile([P, BLOCKS], F32)
+        late_cols = keep.tile([P, 2 * BLOCKS], F32)
+        gamma = late_cols[:, 0:BLOCKS]
+        beta = late_cols[:, BLOCKS : 2 * BLOCKS]
 
         def small(name):
             return keep.tile([P, BLOCKS], F32, name=name)
@@ -141,49 +137,44 @@ def tile_batchedgraphsagemean1_pb_kernel(
         total_r, total_rr, mean, mean_sq, second = small("total_r"), small("total_rr"), small("mean"), small("mean_sq"), small("second")
         var_eps, inv_std, gain, mean_gain, shift = small("var_eps"), small("inv_std"), small("gain"), small("mean_gain"), small("shift")
 
+        def rows_of(g):
+            return slice(g * GROUP_ROWS, (g + 1) * GROUP_ROWS)
+
         with tc.psum_pool(name="psum", bufs=1) as psum:
-            grouped = {}
-            operands = {}
-            squares = {}
-            row_sums = {}
-            inv_norm = {}
-            spread = {}
+            xts, grouped, operands, accs, squares, row_sums, inv_norm, spread, yts, staged = {}, {}, {}, {}, {}, {}, {}, {}, {}, {}
 
-            def transpose_vectors():
-                vec_f32 = keep.tile([P, P], F32)
-                nc.vector.tensor_copy(out=vec_f32[:], in_=vec_rows[:])
-                vec_ps = psum.tile([P, P], F32, tag="xt", bufs=2)
+            def transpose_vectors(rows, cols):
+                vec_f32 = work.tile([P, P], F32, name="vec_f32", bufs=1)
+                nc.vector.tensor_copy(out=vec_f32[:], in_=rows[:])
+                vec_ps = psum.tile([P, P], F32, tag="acc", bufs=3)
                 nc.tensor.transpose(vec_ps[:], vec_f32[:], ident[:])
-                nc.vector.tensor_copy(out=vec_cols[:], in_=vec_ps[:, 0 : 3 * BLOCKS])
+                nc.vector.tensor_copy(out=cols[:], in_=vec_ps[:, 0 : cols.shape[1]])
 
-            def transpose_half(q):
-                m, half = q // 2, q % 2
-                g, s = m // STREAMS, m % STREAMS
-                if half == 0:
-                    grouped[m] = work.tile([P, GROUP_ROWS, 2], F32, name="grouped", bufs=5, align_bytes=64)
+            def transpose_half(g, s, t):
+                if t == 0:
+                    grouped[g, s] = work.tile([P, GROUP_ROWS, 2], F32, name="grouped", bufs=4, align_bytes=64)
                 xt = psum.tile([P, 2, HALF_TILES * P], F32, tag="xt", bufs=2)
                 for i in range(HALF_TILES):
-                    words = x_raw[:, s, g * GROUP_TILES + half * HALF_TILES + i, :].bitcast(F32)
+                    words = x_raw[:, s, g * GROUP_TILES + t + i, :].bitcast(F32)
                     for u in range(2):
                         nc.tensor.transpose(xt[:, u, i * P : (i + 1) * P], words[:, u : K // 2 : 2], ident[:])
-                rows = slice(half * HALF_TILES * P, (half + 1) * HALF_TILES * P)
-                nc.scalar.copy(out=grouped[m][:, rows, :], in_=xt[:].rearrange("p u r -> p r u"))
+                xts[g, s, t] = xt
 
-            def quantise(m):
+            def copy_half(g, s, t):
+                nc.scalar.copy(out=grouped[g, s][:, t * P : (t + HALF_TILES) * P, :], in_=xts[g, s, t][:].rearrange("p u r -> p r u"))
+
+            def quantise(g, s):
                 codes = work.tile([P, GROUP_ROWS], U32, tag="codes", bufs=OPERANDS, align_bytes=64)
                 plane = work.tile([P, GROUP_ROWS], U8, tag="plane", bufs=OPERANDS, align_bytes=64)
                 nc.vector.quantize_mx(
-                    out=codes[:].bitcast(FP8X4),
-                    scales=plane[:],
-                    in_=grouped[m][:].rearrange("p r u -> p (r u)").bitcast(BF16),
+                    out=codes[:].bitcast(FP8X4), scales=plane[:], in_=grouped[g, s][:].rearrange("p r u -> p (r u)").bitcast(BF16)
                 )
-                operands[m] = (codes, plane)
+                operands[g, s] = (codes, plane)
 
-            def project(i):
-                g, c = i // BLOCKS, i % BLOCKS
+            def project(g, c):
                 s = c // STREAM_BLOCKS
                 cols = slice((c % STREAM_BLOCKS) * P, (c % STREAM_BLOCKS + 1) * P)
-                codes, plane = operands[g * STREAMS + s]
+                codes, plane = operands[g, s]
                 acc = psum.tile([P, GROUP_ROWS], F32, tag="acc", bufs=3)
                 nc.tensor.matmul_mx(
                     out=acc[:],
@@ -194,26 +185,31 @@ def tile_batchedgraphsagemean1_pb_kernel(
                     start=True,
                     stop=True,
                 )
-                h = h_all[:, g, c, :]
-                if c in SCALAR_EMPTIES:
-                    nc.scalar.activation(out=h, in_=acc[:], func=ACT.Identity, bias=bias[:, c : c + 1])
-                else:
-                    nc.vector.tensor_scalar_add(out=h, in0=acc[:], scalar1=bias[:, c : c + 1])
-                squares[i] = work.tile([P, GROUP_ROWS], F32, name="squares", bufs=SUM_LAG + 2)
-                if c in SCALAR_SQUARES:
-                    nc.scalar.activation(out=squares[i][:], in_=h, func=ACT.Square)
-                else:
-                    nc.gpsimd.tensor_tensor(out=squares[i][:], in0=h, in1=h, op=ALU.mult)
+                accs[g, c] = acc
 
-            def sum_squares(i):
-                g, c = i // BLOCKS, i % BLOCKS
+            def empty(g, c):
+                h = h_all[:, c, rows_of(g)]
+                if c in SCALAR_EMPTIES[g]:
+                    nc.scalar.activation(out=h, in_=accs[g, c][:], func=ACT.Identity, bias=bias[:, c : c + 1])
+                else:
+                    nc.vector.tensor_scalar_add(out=h, in0=accs[g, c][:], scalar1=bias[:, c : c + 1])
+
+            def square(g, c):
+                h = h_all[:, c, rows_of(g)]
+                squares[g, c] = work.tile([P, GROUP_ROWS], F32, name="squares", bufs=12)
+                if c in SCALAR_SQUARES[g]:
+                    nc.scalar.activation(out=squares[g, c][:], in_=h, func=ACT.Square)
+                else:
+                    nc.gpsimd.tensor_tensor(out=squares[g, c][:], in0=h, in1=h, op=ALU.mult)
+
+            def sum_squares(g, c):
                 if c == 0:
                     sums = psum.tile([P, GROUP_TILES, P], F32, tag="row_sums", bufs=1)
                     row_sums[g] = sums
                 for t in range(GROUP_TILES):
                     nc.tensor.matmul(
                         out=row_sums[g][:, t, :],
-                        lhsT=squares[i][:, t * P : (t + 1) * P],
+                        lhsT=squares[g, c][:, t * P : (t + 1) * P],
                         rhs=ident[:],
                         is_transpose=True,
                         start=(c == 0 and t == 0),
@@ -230,45 +226,51 @@ def tile_batchedgraphsagemean1_pb_kernel(
                 nc.scalar.activation(out=inv_norm[g][:], in_=inv_norm[g][:], func=ACT.Abs_reciprocal_sqrt)
 
             def spread_norms(g):
-                spread[g] = psum.tile([P, GROUP_ROWS], F32, name="spread", bufs=2)
+                spread[g] = psum.tile([P, GROUP_ROWS], F32, name="spread", tag="spread" if g < GROUPS - 2 else "xt", bufs=2)
                 for t in range(GROUP_TILES):
-                    nc.tensor.transpose(
-                        spread[g][:, t * P : (t + 1) * P], inv_norm[g][:, t : t + 1].to_broadcast([P, P]), ident[:]
-                    )
+                    nc.tensor.transpose(spread[g][:, t * P : (t + 1) * P], inv_norm[g][:, t : t + 1].to_broadcast([P, P]), ident[:])
 
-            def normalise(i):
-                g, c = i // BLOCKS, i % BLOCKS
-                r = h_all[:, g, c, :]
+            def normalise(g, c):
+                r = h_all[:, c, rows_of(g)]
                 nc.vector.scalar_tensor_tensor(
-                    out=r,
-                    in0=r,
-                    scalar=0.0,
-                    in1=spread[g][:],
-                    op0=ALU.max,
-                    op1=ALU.mult,
-                    accum_out=sum_r[:, c, g : g + 1],
+                    out=r, in0=r, scalar=0.0, in1=spread[g][:], op0=ALU.max, op1=ALU.mult, accum_out=sum_r[:, c, g : g + 1]
                 )
+
+            def square_r(g, c):
                 unread = work.tile([P, GROUP_ROWS], F32, tag="unread", bufs=2)
-                nc.scalar.activation(out=unread[:], in_=r, func=ACT.Square, accum_out=sum_rr[:, c, g : g + 1])
+                nc.scalar.activation(out=unread[:], in_=h_all[:, c, rows_of(g)], func=ACT.Square, accum_out=sum_rr[:, c, g : g + 1])
 
             def statistics(s):
                 cs = slice(s * STREAM_BLOCKS, (s + 1) * STREAM_BLOCKS)
-                nc.vector.tensor_reduce(out=total_r[:, cs], in_=sum_r[:, cs, :], axis=AXIS.X, op=ALU.add)
-                nc.vector.tensor_scalar_mul(out=mean[:, cs], in0=total_r[:, cs], scalar1=1.0 / ROWS)
-                nc.vector.tensor_mul(out=mean_sq[:, cs], in0=mean[:, cs], in1=mean[:, cs])
-                nc.vector.tensor_reduce(out=total_rr[:, cs], in_=sum_rr[:, cs, :], axis=AXIS.X, op=ALU.add)
-                nc.vector.tensor_scalar(
-                    out=second[:, cs], in0=total_rr[:, cs], scalar1=1.0 / ROWS, scalar2=BN_EPS, op0=ALU.mult, op1=ALU.add
-                )
-                nc.vector.tensor_sub(out=var_eps[:, cs], in0=second[:, cs], in1=mean_sq[:, cs])
-                nc.scalar.activation(out=inv_std[:, cs], in_=var_eps[:, cs], func=ACT.Abs_reciprocal_sqrt)
-                nc.vector.tensor_mul(out=gain[:, cs], in0=gamma[:, cs], in1=inv_std[:, cs])
-                nc.vector.tensor_mul(out=mean_gain[:, cs], in0=mean[:, cs], in1=gain[:, cs])
-                nc.vector.tensor_sub(out=shift[:, cs], in0=beta[:, cs], in1=mean_gain[:, cs])
+
+                def total(out, sums):
+                    nc.vector.tensor_reduce(out=out[:, cs], in_=sums[:, cs, :], axis=AXIS.X, op=ALU.add)
+
+                def scale(out, in_, factor, offset):
+                    nc.gpsimd.tensor_scalar(out=out[:, cs], in0=in_[:, cs], scalar1=factor, scalar2=offset, op0=ALU.mult, op1=ALU.add)
+
+                def combine(out, in0, in1, op):
+                    nc.gpsimd.tensor_tensor(out=out[:, cs], in0=in0[:, cs], in1=in1[:, cs], op=op)
+
+                def invert():
+                    nc.scalar.activation(out=inv_std[:, cs], in_=var_eps[:, cs], func=ACT.Abs_reciprocal_sqrt)
+
+                return [
+                    (total, total_r, sum_r),
+                    (scale, mean, total_r, 1.0 / ROWS, 0.0),
+                    (combine, mean_sq, mean, mean, ALU.mult),
+                    (total, total_rr, sum_rr),
+                    (scale, second, total_rr, 1.0 / ROWS, BN_EPS),
+                    (combine, var_eps, second, mean_sq, ALU.subtract),
+                    (invert,),
+                    (combine, gain, gamma, inv_std, ALU.mult),
+                    (combine, mean_gain, mean, gain, ALU.mult),
+                    (combine, shift, beta, mean_gain, ALU.subtract),
+                ]
 
             def scale_and_shift(g, c):
-                y = h_all[:, g, c, :]
-                engine = c % 3
+                y = h_all[:, c, rows_of(g)]
+                engine = (0, 1, 2, 2)[c % 4]
                 if engine == 0:
                     nc.vector.tensor_scalar(
                         out=y, in0=y, scalar1=gain[:, c : c + 1], scalar2=shift[:, c : c + 1], op0=ALU.mult, op1=ALU.add
@@ -280,70 +282,99 @@ def tile_batchedgraphsagemean1_pb_kernel(
                         out=y, in0=y, scalar1=gain[:, c : c + 1], scalar2=shift[:, c : c + 1], op0=ALU.mult, op1=ALU.add
                     )
 
-            def store_tile(s, g, t):
-                number = (s * GROUPS + g) * GROUP_TILES + t
-                if t % 2 == 0:
-                    slot = number // 2 % STAGING_SLOTS
-                    staged[s, g, t // 2] = staging[:, slot * SLOT_WORDS : (slot + 1) * SLOT_WORDS].bitcast(F32).rearrange("p (t c) -> p t c", t=2)
+            def transpose_out(s, n):
+                number = s * ROW_TILES + n
                 tag, bufs = YT_BANKS[number % len(YT_BANKS)]
                 yt = psum.tile([P, STREAM_CHANNELS], F32, tag=tag, bufs=bufs)
                 for j in range(STREAM_BLOCKS):
-                    nc.tensor.transpose(
-                        yt[:, j * P : (j + 1) * P], h_all[:, g, s * STREAM_BLOCKS + j, t * P : (t + 1) * P], ident[:]
+                    nc.tensor.transpose(yt[:, j * P : (j + 1) * P], h_all[:, s * STREAM_BLOCKS + j, n * P : (n + 1) * P], ident[:])
+                yts[number] = yt
+
+            def land(s, n):
+                number = s * ROW_TILES + n
+                if n % 2 == 0:
+                    slot = number // 2 % STAGING_SLOTS
+                    staged[number // 2] = (
+                        staging[:, slot * SLOT_WORDS : (slot + 1) * SLOT_WORDS].bitcast(F32).rearrange("p (t c) -> p t c", t=2)
                     )
-                landing = staged[s, g, t // 2][:, t % 2, :]
+                landing = staged[number // 2][:, n % 2, :]
                 if number % 2 == 0:
-                    nc.vector.tensor_copy(out=landing, in_=yt[:])
+                    nc.vector.tensor_copy(out=landing, in_=yts[number][:])
                 else:
-                    nc.scalar.copy(out=landing, in_=yt[:])
-                if t % 2 == 1:
-                    row0 = g * GROUP_TILES + t - 1
+                    nc.scalar.copy(out=landing, in_=yts[number][:])
+                if number in STORED_ALONE:
+                    stored = 1
+                else:
+                    stored = 2 * (n % 2)
+                if stored:
                     nc.sync.dma_start(
-                        out=out_rows[:, row0 : row0 + 2, s * STREAM_CHANNELS : (s + 1) * STREAM_CHANNELS], in_=staged[s, g, t // 2]
+                        out=out_rows[:, n + 1 - stored : n + 1, s * STREAM_CHANNELS : (s + 1) * STREAM_CHANNELS],
+                        in_=staged[number // 2][:, n % 2 + 1 - stored : n % 2 + 1, :],
                     )
 
-            def finish_items(s):
-                items = [(scale_and_shift, 0, s * STREAM_BLOCKS + j) for j in range(STREAM_BLOCKS)]
-                for g in range(GROUPS):
-                    for t in range(GROUP_TILES):
-                        if g + 1 < GROUPS:
-                            items.append((scale_and_shift, g + 1, s * STREAM_BLOCKS + t))
-                        items.append((store_tile, s, g, t))
-                return items
+            calls = []
 
-            half_at = {}
-            for q in range(HALVES):
-                half_at[2 * (min(q, FIRST_HALVES) - HALVES_AHEAD) + max(q - FIRST_HALVES, 0)] = q
-            staged = {}
-            waiting = []
-            for step in range(-2 * HALVES_AHEAD, TILES + APPLY_LAG):
-                if step == -1:
-                    transpose_vectors()
-                for g in range(GROUPS):
-                    if step == g * BLOCKS + FLOOR_AT:
-                        floor_sums(g)
-                    if step == g * BLOCKS + RSQRT_AT:
-                        invert_norms(g)
-                    if step == g * BLOCKS + SPREAD_AT:
-                        spread_norms(g)
-                if step in half_at:
-                    transpose_half(half_at[step])
-                q = half_at.get(step - QUANT_LAG, 0)
-                if q % 2 == 1:
-                    quantise(q // 2)
-                if 0 <= step < TILES:
-                    project(step)
-                if 0 <= step - SUM_LAG < TILES:
-                    sum_squares(step - SUM_LAG)
-                if 0 <= step - APPLY_LAG:
-                    normalise(step - APPLY_LAG)
-                    done_tiles = step - APPLY_LAG - (TILES - BLOCKS) + 1
-                    if done_tiles > 0 and done_tiles % STREAM_BLOCKS == 0:
-                        s = done_tiles // STREAM_BLOCKS - 1
-                        statistics(s)
-                        waiting.extend(finish_items(s))
-                    for item in waiting[:ITEMS_A_STEP]:
-                        item[0](*item[1:])
-                    waiting[:ITEMS_A_STEP] = []
-            for item in waiting:
-                item[0](*item[1:])
+            def at(time, call, *args):
+                calls.append((time, len(calls), call, args))
+
+            at(-2, transpose_vectors, bias_rows, bias)
+            at(2 * BLOCKS, transpose_vectors, late_rows, late_cols)
+            for q, (g, s, t) in enumerate(HALVES):
+                time = 2 * (q - HALVES_AHEAD)
+                at(time, transpose_half, g, s, t)
+                at(time + COPY_LAG, copy_half, g, s, t)
+                if t == GROUP_TILES - HALF_TILES:
+                    at(time + QUANT_LAG, quantise, g, s)
+
+            def sum_lag(run):
+                if run < BLOCKS:
+                    return FIRST_SUM_LAG
+                return SUM_LAG - (SUM_LAG - LAST_SUM_LAG) * max(run - STEPS + BLOCKS + 1, 0) / BLOCKS
+
+            normalised = {}
+            for g in range(GROUPS):
+                for c in range(BLOCKS):
+                    tile = g * BLOCKS + c
+                    run = tile // RUN * RUN
+                    summed = run + sum_lag(run)
+                    at(run, project, g, c)
+                    at(tile + EMPTY_LAG, empty, g, c)
+                    at(tile + SQUARE_LAG, square, g, c)
+                    at(summed, sum_squares, g, c)
+                at(summed + CHAIN_LAG, floor_sums, g)
+                at(summed + 2 * CHAIN_LAG, invert_norms, g)
+                at(summed + 3 * CHAIN_LAG, spread_norms, g)
+                first = summed + 3 * CHAIN_LAG + APPLY_LAG
+                for c in range(BLOCKS):
+                    if g < DEFER_FROM[c // STREAM_BLOCKS]:
+                        time = first + (c if g < GROUPS - 1 else c * FAST)
+                        normalised[g, c] = min(time, max(first, STEPS) + (time - max(first, STEPS)) * FAST) if time > STEPS else time
+            barrier = max(normalised[GROUPS - 1, c] for c in range(STREAM_BLOCKS)) + FAST + SQUARE_R_LAG
+            for s in range(1, STREAMS):
+                time = barrier + DEFER_LAG[s]
+                for g in range(DEFER_FROM[s], GROUPS):
+                    for c in range(s * STREAM_BLOCKS, (s + 1) * STREAM_BLOCKS):
+                        normalised[g, c] = time
+                        time += DEFER_PACE[s]
+            free = 0
+            for s in range(STREAMS):
+                summed = 0
+                for c in range(s * STREAM_BLOCKS, (s + 1) * STREAM_BLOCKS):
+                    for g in range(GROUPS):
+                        time = normalised[g, c]
+                        at(time, normalise, g, c)
+                        at(time + SQUARE_R_LAG, square_r, g, c)
+                        summed = max(summed, time + SQUARE_R_LAG + FAST)
+                for call, *args in statistics(s):
+                    at(summed, call, *args)
+                    summed += STAT_LAG
+                first = max(free, summed)
+                free = first + STORE_PACE * ROW_TILES
+                for n in range(ROW_TILES):
+                    g, j = n // GROUP_TILES, n % GROUP_TILES
+                    at(first + STORE_PACE * max(n - 2.5, 0), scale_and_shift, g, s * STREAM_BLOCKS + j)
+                    at(first + STORE_PACE * n + OUT_LAG, transpose_out, s, n)
+                    at(first + STORE_PACE * n + OUT_LAG + LAND_LAG, land, s, n)
+            with tc.manual_schedule():
+                for time, n, call, args in sorted(calls, key=lambda entry: entry[:2]):
+                    call(*args)

@@ -42,20 +42,21 @@ SUM_LAG = 9
 LAST_SUM_LAG = 3
 CHAIN_LAG = 0.7
 APPLY_LAG = 1
-SQUARE_R_LAG = 1
-STAT_LAG = 0.5
-STORE_PACE = 0.4
+SQUARE_R_LAG = 1.2
+STAT_LAGS = (0.5, 0.3, 0.3)
+STORE_PACE = 0.45
 LAND_LAG = 1
 FAST = 0.6
 DEFER_FROM = (GROUPS, 3, 2)
-DEFER_LAG = (0, 1, 0.5)
-DEFER_PACE = (0, 1, 1.8)
+DEFER_LAG = (0, 2.5, 0)
+DEFER_PACE = (0, 1, 2)
 OUT_LAG = 0.3
 
-SCALAR_EMPTIES = ((1, 4, 6, 9, 11), (1, 4, 6, 9, 11), (1, 4, 6, 9, 11), (1, 4, 6, 9, 11))
-SCALAR_SQUARES = ((1,4,6,9,11), (0,3,6,9), (3, 7, 10), (3,10))
+SCALAR_EMPTIES = ((1, 4, 6, 9, 11), (1, 4, 6, 9, 11), (1, 4, 6, 9, 11), (1, 3, 5, 7, 9, 11))
+SCALAR_SQUARES = ((0, 2, 4, 6, 8, 10), (0, 2, 4, 6, 8, 10), (3, 7, 10), (3, 7, 10))
 YT_BANKS = (("acc", 3), ("spread", 2), ("acc", 3), ("spread", 2), ("acc", 3), ("row_sums", 1))
 STAGING_SLOTS = 12
+TENSOR_SCALES = (0, 4)
 STORED_ALONE = (0, 1)
 SLOT_WORDS = 2048
 
@@ -134,8 +135,10 @@ def tile_batchedgraphsagemean1_pb_kernel(
         def small(name):
             return keep.tile([P, BLOCKS], F32, name=name)
 
-        total_r, total_rr, mean, mean_sq, second = small("total_r"), small("total_rr"), small("mean"), small("mean_sq"), small("second")
-        var_eps, inv_std, gain, mean_gain, shift = small("var_eps"), small("inv_std"), small("gain"), small("mean_gain"), small("shift")
+        total_r, total_rr, minus_mean_sq, var = small("total_r"), small("total_rr"), small("minus_mean_sq"), small("var")
+        inv_std, gain, minus_mean_gain, shift = small("inv_std"), small("gain"), small("minus_mean_gain"), small("shift")
+        eps = keep.tile([P, 1], F32)
+        nc.vector.tensor_scalar_mul(out=eps[:], in0=ones[:], scalar1=BN_EPS)
 
         def rows_of(g):
             return slice(g * GROUP_ROWS, (g + 1) * GROUP_ROWS)
@@ -246,31 +249,26 @@ def tile_batchedgraphsagemean1_pb_kernel(
                 def total(out, sums):
                     nc.vector.tensor_reduce(out=out[:, cs], in_=sums[:, cs, :], axis=AXIS.X, op=ALU.add)
 
-                def scale(out, in_, factor, offset):
-                    nc.gpsimd.tensor_scalar(out=out[:, cs], in0=in_[:, cs], scalar1=factor, scalar2=offset, op0=ALU.mult, op1=ALU.add)
-
-                def combine(out, in0, in1, op):
-                    nc.gpsimd.tensor_tensor(out=out[:, cs], in0=in0[:, cs], in1=in1[:, cs], op=op)
+                def combine(out, in0, factor, in1, op):
+                    nc.vector.scalar_tensor_tensor(out=out[:, cs], in0=in0[:, cs], scalar=factor, in1=in1[:, cs], op0=ALU.mult, op1=op)
 
                 def invert():
-                    nc.scalar.activation(out=inv_std[:, cs], in_=var_eps[:, cs], func=ACT.Abs_reciprocal_sqrt)
+                    nc.scalar.activation(out=inv_std[:, cs], in_=var[:, cs], func=ACT.Abs_reciprocal_sqrt, bias=eps[:])
 
                 return [
                     (total, total_r, sum_r),
-                    (scale, mean, total_r, 1.0 / ROWS, 0.0),
-                    (combine, mean_sq, mean, mean, ALU.mult),
+                    (combine, minus_mean_sq, total_r, -1.0 / (ROWS * ROWS), total_r, ALU.mult),
                     (total, total_rr, sum_rr),
-                    (scale, second, total_rr, 1.0 / ROWS, BN_EPS),
-                    (combine, var_eps, second, mean_sq, ALU.subtract),
+                    (combine, var, total_rr, 1.0 / ROWS, minus_mean_sq, ALU.add),
                     (invert,),
-                    (combine, gain, gamma, inv_std, ALU.mult),
-                    (combine, mean_gain, mean, gain, ALU.mult),
-                    (combine, shift, beta, mean_gain, ALU.subtract),
+                    (combine, gain, gamma, 1.0, inv_std, ALU.mult),
+                    (combine, minus_mean_gain, total_r, -1.0 / ROWS, gain, ALU.mult),
+                    (combine, shift, beta, 1.0, minus_mean_gain, ALU.add),
                 ]
 
             def scale_and_shift(g, c):
                 y = h_all[:, c, rows_of(g)]
-                engine = (0, 1, 2, 2)[c % 4]
+                engine = (0, 1, 2, 2)[c % STREAM_BLOCKS]
                 if engine == 0:
                     nc.vector.tensor_scalar(
                         out=y, in0=y, scalar1=gain[:, c : c + 1], scalar2=shift[:, c : c + 1], op0=ALU.mult, op1=ALU.add
@@ -282,12 +280,24 @@ def tile_batchedgraphsagemean1_pb_kernel(
                         out=y, in0=y, scalar1=gain[:, c : c + 1], scalar2=shift[:, c : c + 1], op0=ALU.mult, op1=ALU.add
                     )
 
+            diagonals = {}
+
+            def make_diagonal(c):
+                diagonals[c] = work.tile([P, P], F32, name="diagonal", bufs=2)
+                nc.gpsimd.tensor_scalar(out=diagonals[c][:], in0=ident[:], scalar1=gain[:, c : c + 1], scalar2=0.0, op0=ALU.mult, op1=ALU.add)
+
             def transpose_out(s, n):
                 number = s * ROW_TILES + n
                 tag, bufs = YT_BANKS[number % len(YT_BANKS)]
                 yt = psum.tile([P, STREAM_CHANNELS], F32, tag=tag, bufs=bufs)
                 for j in range(STREAM_BLOCKS):
-                    nc.tensor.transpose(yt[:, j * P : (j + 1) * P], h_all[:, s * STREAM_BLOCKS + j, n * P : (n + 1) * P], ident[:])
+                    c = s * STREAM_BLOCKS + j
+                    r = h_all[:, c, n * P : (n + 1) * P]
+                    if c in TENSOR_SCALES:
+                        nc.tensor.matmul(out=yt[:, j * P : (j + 1) * P], lhsT=shift[:, c : c + 1].to_broadcast([P, P]), rhs=ident[:], is_transpose=True, start=True, stop=False)
+                        nc.tensor.matmul(out=yt[:, j * P : (j + 1) * P], lhsT=r, rhs=diagonals[c][:], start=False, stop=True)
+                    else:
+                        nc.tensor.transpose(yt[:, j * P : (j + 1) * P], r, ident[:])
                 yts[number] = yt
 
             def land(s, n):
@@ -298,7 +308,7 @@ def tile_batchedgraphsagemean1_pb_kernel(
                         staging[:, slot * SLOT_WORDS : (slot + 1) * SLOT_WORDS].bitcast(F32).rearrange("p (t c) -> p t c", t=2)
                     )
                 landing = staged[number // 2][:, n % 2, :]
-                if number % 2 == 0:
+                if number % 5 in (0, 2, 4):
                     nc.vector.tensor_copy(out=landing, in_=yts[number][:])
                 else:
                     nc.scalar.copy(out=landing, in_=yts[number][:])
@@ -367,12 +377,16 @@ def tile_batchedgraphsagemean1_pb_kernel(
                         summed = max(summed, time + SQUARE_R_LAG + FAST)
                 for call, *args in statistics(s):
                     at(summed, call, *args)
-                    summed += STAT_LAG
+                    summed += STAT_LAGS[s]
                 first = max(free, summed)
                 free = first + STORE_PACE * ROW_TILES
                 for n in range(ROW_TILES):
                     g, j = n // GROUP_TILES, n % GROUP_TILES
-                    at(first + STORE_PACE * max(n - 2.5, 0), scale_and_shift, g, s * STREAM_BLOCKS + j)
+                    c = s * STREAM_BLOCKS + j
+                    if c not in TENSOR_SCALES:
+                        at(first + STORE_PACE * max(n - 2.5, 0), scale_and_shift, g, c)
+                    elif g == 0:
+                        at(first, make_diagonal, c)
                     at(first + STORE_PACE * n + OUT_LAG, transpose_out, s, n)
                     at(first + STORE_PACE * n + OUT_LAG + LAND_LAG, land, s, n)
             with tc.manual_schedule():

import concourse.mybir as mybir
from concourse.masks import make_identity

F32 = mybir.dt.float32
BF16 = mybir.dt.bfloat16
I32 = mybir.dt.int32
U32 = mybir.dt.uint32
U8 = mybir.dt.uint8
FP8X4 = mybir.dt.float8_e4m3fn_x4
ALU = mybir.AluOpType
ACT = mybir.ActivationFunctionType
AXIS = mybir.AxisListType

P = 128
ROWS = 2048
K = 512
STREAMS = 3
STREAM_CHANNELS = 512
CHANNELS = STREAMS * STREAM_CHANNELS
BLOCKS = CHANNELS // P
STREAM_BLOCKS = STREAM_CHANNELS // P
ROW_TILES = ROWS // P
GROUP_TILES = 4
GROUP_ROWS = GROUP_TILES * P
GROUPS = ROW_TILES // GROUP_TILES
STEPS = GROUPS * BLOCKS
OPERANDS = GROUPS * STREAMS
HALF_TILES = 2
HALVES = [(g, s, t) for g in range(GROUPS) for s in range(STREAMS) for t in range(0, GROUP_TILES, HALF_TILES)]
SCALE_ROWS = K // 32
NORM_FLOOR = 1e-12
BN_EPS = 1e-5

RUN = 2
HALVES_AHEAD = 8 / 2
COPY_LAG = 1.5
QUANT_LAG = 3
EMPTY_LAG = 0.4
SQUARE_LAG = 1.6
FIRST_SUM_LAG = 7
SUM_LAG = 9
LAST_SUM_LAG = 3
CHAIN_LAG = 0.7
APPLY_LAG = 1
SQUARE_R_LAG = 1.2
STAT_LAGS = (0.5, 0.3, 0.3)
STORE_PACE = 0.45
LAND_LAG = 1
FAST = 0.6
DEFER_FROM = (GROUPS, 3, 2)
DEFER_LAG = (0, 2.5, 0)
DEFER_PACE = (0, 1, 2)
OUT_LAG = 0.3

SCALAR_EMPTIES = ((1, 4, 6, 9, 11), (1, 4, 6, 9, 11), (1, 4, 6, 9, 11), (1, 3, 5, 7, 9, 11))
SCALAR_SQUARES = ((0, 2, 4, 6, 8, 10), (0, 2, 4, 6, 8, 10), (3, 7, 10), (3, 7, 10))
YT_BANKS = (("acc", 3), ("spread", 2), ("acc", 3), ("spread", 2), ("acc", 3), ("row_sums", 1))
STAGING_SLOTS = 12
TENSOR_SCALES = (0, 4)
STORED_ALONE = (0, 1)
SLOT_WORDS = 2048

FLOPS = 2 * ROWS * K * CHANNELS


def tile_batchedgraphsagemean1_pb_kernel(
    tc, x, nb, mu, Wx_w_words, Wx_w_scales, Wx_b, Wn_w_words, Wn_w_scales, Wn_b, Wr_w_words, Wr_w_scales, Wr_b, bn_gamma, bn_beta, out
):
    nc = tc.nc
    streams = [src.flatten_outer_dims().rearrange("(p n) k -> p n k", n=ROW_TILES) for src in (x, nb, mu)]
    weight_words = [Wx_w_words, Wn_w_words, Wr_w_words]
    weight_scales = [Wx_w_scales, Wn_w_scales, Wr_w_scales]
    out_rows = out.flatten_outer_dims().rearrange("(p n) c -> p n c", n=ROW_TILES)

    with tc.tile_pool(name="keep", bufs=1) as keep, tc.tile_pool(name="work", bufs=2) as work:
        ident = keep.tile([P, P], F32)
        make_identity(nc, ident[:])
        ones = keep.tile([P, 1], F32)
        nc.vector.memset(ones[:], 1.0)
        w_codes = keep.tile([P, STREAMS, STREAM_CHANNELS], U32, align_bytes=64)
        w_planes = keep.tile([P, STREAMS, STREAM_CHANNELS], U8, align_bytes=64)
        bias_rows = keep.tile([P, P], BF16)
        nc.vector.memset(bias_rows[:], 0.0)
        late_rows = keep.tile([P, P], BF16)
        nc.vector.memset(late_rows[:], 0.0)
        nc.vector.memset(w_planes[:].bitcast(I32), 0)

        def load_vectors(rows, vecs, queue):
            first_row = 0
            for vec in vecs:
                n_rows = vec.shape[0] // P
                queue.dma_start(out=rows[first_row : first_row + n_rows, :], in_=vec.rearrange("(r c) -> r c", c=P))
                first_row += n_rows

        load_vectors(bias_rows, (Wx_b, Wn_b, Wr_b), nc.scalar)
        table_warm = keep.tile([P, 1], F32)
        nc.scalar.activation(out=table_warm[:], in_=ones[:, 0:1], func=ACT.Abs_reciprocal_sqrt)
        x_raw = keep.tile([P, STREAMS, ROW_TILES, K], BF16)

        def load_weight(s):
            nc.sync.dma_start(
                out=w_codes[:, s, :].bitcast(I32), in_=weight_words[s][0].rearrange("p n t -> p (n t)").bitcast(I32)
            )

        def load_planes(s):
            for quadrant in range(SCALE_ROWS // 4):
                nc.sync.dma_start(
                    out=w_planes[32 * quadrant : 32 * quadrant + 4, s, :].bitcast(I32),
                    in_=weight_scales[s][0, 4 * quadrant : 4 * quadrant + 4, :].bitcast(I32),
                )

        def load_rows(s, first, n):
            rows = slice(first, first + n)
            nc.sync.dma_start(out=x_raw[:, s, rows, :], in_=streams[s][:, rows, :])

        for s in range(STREAMS):
            load_rows(s, 0, 2)
            load_rows(s, 2, 2)
            load_weight(s)
            load_planes(s)
        for g in range(1, GROUPS):
            for s in range(STREAMS):
                for t in range(0, GROUP_TILES, HALF_TILES):
                    load_rows(s, g * GROUP_TILES + t, HALF_TILES)
        load_vectors(late_rows, (bn_gamma, bn_beta), nc.sync)
        staging = x_raw[:].rearrange("p s n k -> p (s n k)")
        h_all = keep.tile([P, BLOCKS, ROWS], F32)
        sum_r = keep.tile([P, BLOCKS, GROUPS], F32)
        sum_rr = keep.tile([P, BLOCKS, GROUPS], F32)
        bias = keep.tile([P, BLOCKS], F32)
        late_cols = keep.tile([P, 2 * BLOCKS], F32)
        gamma = late_cols[:, 0:BLOCKS]
        beta = late_cols[:, BLOCKS : 2 * BLOCKS]

        def small(name):
            return keep.tile([P, BLOCKS], F32, name=name)

        total_r, total_rr, minus_mean_sq, var = small("total_r"), small("total_rr"), small("minus_mean_sq"), small("var")
        inv_std, gain, minus_mean_gain, shift = small("inv_std"), small("gain"), small("minus_mean_gain"), small("shift")
        eps = keep.tile([P, 1], F32)
        nc.vector.tensor_scalar_mul(out=eps[:], in0=ones[:], scalar1=BN_EPS)

        def rows_of(g):
            return slice(g * GROUP_ROWS, (g + 1) * GROUP_ROWS)

        with tc.psum_pool(name="psum", bufs=1) as psum:
            xts, grouped, operands, accs, squares, row_sums, inv_norm, spread, yts, staged = {}, {}, {}, {}, {}, {}, {}, {}, {}, {}

            def transpose_vectors(rows, cols):
                vec_f32 = work.tile([P, P], F32, name="vec_f32", bufs=1)
                nc.vector.tensor_copy(out=vec_f32[:], in_=rows[:])
                vec_ps = psum.tile([P, P], F32, tag="acc", bufs=3)
                nc.tensor.transpose(vec_ps[:], vec_f32[:], ident[:])
                nc.vector.tensor_copy(out=cols[:], in_=vec_ps[:, 0 : cols.shape[1]])

            def transpose_half(g, s, t):
                if t == 0:
                    grouped[g, s] = work.tile([P, GROUP_ROWS, 2], F32, name="grouped", bufs=4, align_bytes=64)
                xt = psum.tile([P, 2, HALF_TILES * P], F32, tag="xt", bufs=2)
                for i in range(HALF_TILES):
                    words = x_raw[:, s, g * GROUP_TILES + t + i, :].bitcast(F32)
                    for u in range(2):
                        nc.tensor.transpose(xt[:, u, i * P : (i + 1) * P], words[:, u : K // 2 : 2], ident[:])
                xts[g, s, t] = xt

            def copy_half(g, s, t):
                nc.scalar.copy(out=grouped[g, s][:, t * P : (t + HALF_TILES) * P, :], in_=xts[g, s, t][:].rearrange("p u r -> p r u"))

            def quantise(g, s):
                codes = work.tile([P, GROUP_ROWS], U32, tag="codes", bufs=OPERANDS, align_bytes=64)
                plane = work.tile([P, GROUP_ROWS], U8, tag="plane", bufs=OPERANDS, align_bytes=64)
                nc.vector.quantize_mx(
                    out=codes[:].bitcast(FP8X4), scales=plane[:], in_=grouped[g, s][:].rearrange("p r u -> p (r u)").bitcast(BF16)
                )
                operands[g, s] = (codes, plane)

            def project(g, c):
                s = c // STREAM_BLOCKS
                cols = slice((c % STREAM_BLOCKS) * P, (c % STREAM_BLOCKS + 1) * P)
                codes, plane = operands[g, s]
                acc = psum.tile([P, GROUP_ROWS], F32, tag="acc", bufs=3)
                nc.tensor.matmul_mx(
                    out=acc[:],
                    lhsT=w_codes[:, s, cols].bitcast(FP8X4),
                    lhsT_scale=w_planes[:, s, cols],
                    rhs=codes[:].bitcast(FP8X4),
                    rhs_scale=plane[:],
                    start=True,
                    stop=True,
                )
                accs[g, c] = acc

            def empty(g, c):
                h = h_all[:, c, rows_of(g)]
                if c in SCALAR_EMPTIES[g]:
                    nc.scalar.activation(out=h, in_=accs[g, c][:], func=ACT.Identity, bias=bias[:, c : c + 1])
                else:
                    nc.vector.tensor_scalar_add(out=h, in0=accs[g, c][:], scalar1=bias[:, c : c + 1])

            def square(g, c):
                h = h_all[:, c, rows_of(g)]
                squares[g, c] = work.tile([P, GROUP_ROWS], F32, name="squares", bufs=12)
                if c in SCALAR_SQUARES[g]:
                    nc.scalar.activation(out=squares[g, c][:], in_=h, func=ACT.Square)
                else:
                    nc.gpsimd.tensor_tensor(out=squares[g, c][:], in0=h, in1=h, op=ALU.mult)

            def sum_squares(g, c):
                if c == 0:
                    sums = psum.tile([P, GROUP_TILES, P], F32, tag="row_sums", bufs=1)
                    row_sums[g] = sums
                for t in range(GROUP_TILES):
                    nc.tensor.matmul(
                        out=row_sums[g][:, t, :],
                        lhsT=squares[g, c][:, t * P : (t + 1) * P],
                        rhs=ident[:],
                        is_transpose=True,
                        start=(c == 0 and t == 0),
                        stop=(c == BLOCKS - 1 and t == GROUP_TILES - 1),
                    )

            def floor_sums(g):
                norm_sq = work.tile([P, GROUP_TILES], F32, name="norm_sq")
                nc.vector.tensor_reduce(out=norm_sq[:], in_=row_sums[g][:], axis=AXIS.X, op=ALU.add)
                inv_norm[g] = work.tile([P, GROUP_TILES], F32, name="inv_norm")
                nc.vector.tensor_scalar_max(out=inv_norm[g][:], in0=norm_sq[:], scalar1=NORM_FLOOR * NORM_FLOOR)

            def invert_norms(g):
                nc.scalar.activation(out=inv_norm[g][:], in_=inv_norm[g][:], func=ACT.Abs_reciprocal_sqrt)

            def spread_norms(g):
                spread[g] = psum.tile([P, GROUP_ROWS], F32, name="spread", tag="spread" if g < GROUPS - 2 else "xt", bufs=2)
                for t in range(GROUP_TILES):
                    nc.tensor.transpose(spread[g][:, t * P : (t + 1) * P], inv_norm[g][:, t : t + 1].to_broadcast([P, P]), ident[:])

            def normalise(g, c):
                r = h_all[:, c, rows_of(g)]
                nc.vector.scalar_tensor_tensor(
                    out=r, in0=r, scalar=0.0, in1=spread[g][:], op0=ALU.max, op1=ALU.mult, accum_out=sum_r[:, c, g : g + 1]
                )

            def square_r(g, c):
                unread = work.tile([P, GROUP_ROWS], F32, tag="unread", bufs=2)
                nc.scalar.activation(out=unread[:], in_=h_all[:, c, rows_of(g)], func=ACT.Square, accum_out=sum_rr[:, c, g : g + 1])

            def statistics(s):
                cs = slice(s * STREAM_BLOCKS, (s + 1) * STREAM_BLOCKS)

                def total(out, sums):
                    nc.vector.tensor_reduce(out=out[:, cs], in_=sums[:, cs, :], axis=AXIS.X, op=ALU.add)

                def combine(out, in0, factor, in1, op):
                    nc.vector.scalar_tensor_tensor(out=out[:, cs], in0=in0[:, cs], scalar=factor, in1=in1[:, cs], op0=ALU.mult, op1=op)

                def invert():
                    nc.scalar.activation(out=inv_std[:, cs], in_=var[:, cs], func=ACT.Abs_reciprocal_sqrt, bias=eps[:])

                return [
                    (total, total_r, sum_r),
                    (combine, minus_mean_sq, total_r, -1.0 / (ROWS * ROWS), total_r, ALU.mult),
                    (total, total_rr, sum_rr),
                    (combine, var, total_rr, 1.0 / ROWS, minus_mean_sq, ALU.add),
                    (invert,),
                    (combine, gain, gamma, 1.0, inv_std, ALU.mult),
                    (combine, minus_mean_gain, total_r, -1.0 / ROWS, gain, ALU.mult),
                    (combine, shift, beta, 1.0, minus_mean_gain, ALU.add),
                ]

            def scale_and_shift(g, c):
                y = h_all[:, c, rows_of(g)]
                engine = (0, 1, 2, 2)[c % STREAM_BLOCKS]
                if engine == 0:
                    nc.vector.tensor_scalar(
                        out=y, in0=y, scalar1=gain[:, c : c + 1], scalar2=shift[:, c : c + 1], op0=ALU.mult, op1=ALU.add
                    )
                elif engine == 1:
                    nc.scalar.activation(out=y, in_=y, func=ACT.Identity, scale=gain[:, c : c + 1], bias=shift[:, c : c + 1])
                else:
                    nc.gpsimd.tensor_scalar(
                        out=y, in0=y, scalar1=gain[:, c : c + 1], scalar2=shift[:, c : c + 1], op0=ALU.mult, op1=ALU.add
                    )

            diagonals = {}

            def make_diagonal(c):
                diagonals[c] = work.tile([P, P], F32, name="diagonal", bufs=2)
                nc.gpsimd.tensor_scalar(out=diagonals[c][:], in0=ident[:], scalar1=gain[:, c : c + 1], scalar2=0.0, op0=ALU.mult, op1=ALU.add)

            def transpose_out(s, n):
                number = s * ROW_TILES + n
                tag, bufs = YT_BANKS[number % len(YT_BANKS)]
                yt = psum.tile([P, STREAM_CHANNELS], F32, tag=tag, bufs=bufs)
                for j in range(STREAM_BLOCKS):
                    c = s * STREAM_BLOCKS + j
                    r = h_all[:, c, n * P : (n + 1) * P]
                    if c in TENSOR_SCALES:
                        nc.tensor.matmul(out=yt[:, j * P : (j + 1) * P], lhsT=shift[:, c : c + 1].to_broadcast([P, P]), rhs=ident[:], is_transpose=True, start=True, stop=False)
                        nc.tensor.matmul(out=yt[:, j * P : (j + 1) * P], lhsT=r, rhs=diagonals[c][:], start=False, stop=True)
                    else:
                        nc.tensor.transpose(yt[:, j * P : (j + 1) * P], r, ident[:])
                yts[number] = yt

            def land(s, n):
                number = s * ROW_TILES + n
                if n % 2 == 0:
                    slot = number // 2 % STAGING_SLOTS
                    staged[number // 2] = (
                        staging[:, slot * SLOT_WORDS : (slot + 1) * SLOT_WORDS].bitcast(F32).rearrange("p (t c) -> p t c", t=2)
                    )
                landing = staged[number // 2][:, n % 2, :]
                if number % 5 in (0, 2, 4):
                    nc.vector.tensor_copy(out=landing, in_=yts[number][:])
                else:
                    nc.scalar.copy(out=landing, in_=yts[number][:])
                if number in STORED_ALONE:
                    stored = 1
                else:
                    stored = 2 * (n % 2)
                if stored:
                    nc.sync.dma_start(
                        out=out_rows[:, n + 1 - stored : n + 1, s * STREAM_CHANNELS : (s + 1) * STREAM_CHANNELS],
                        in_=staged[number // 2][:, n % 2 + 1 - stored : n % 2 + 1, :],
                    )

            calls = []

            def at(time, call, *args):
                calls.append((time, len(calls), call, args))

            at(-2, transpose_vectors, bias_rows, bias)
            at(2 * BLOCKS, transpose_vectors, late_rows, late_cols)
            for q, (g, s, t) in enumerate(HALVES):
                time = 2 * (q - HALVES_AHEAD)
                at(time, transpose_half, g, s, t)
                at(time + COPY_LAG, copy_half, g, s, t)
                if t == GROUP_TILES - HALF_TILES:
                    at(time + QUANT_LAG, quantise, g, s)

            def sum_lag(run):
                if run < BLOCKS:
                    return FIRST_SUM_LAG
                return SUM_LAG - (SUM_LAG - LAST_SUM_LAG) * max(run - STEPS + BLOCKS + 1, 0) / BLOCKS

            normalised = {}
            for g in range(GROUPS):
                for c in range(BLOCKS):
                    tile = g * BLOCKS + c
                    run = tile // RUN * RUN
                    summed = run + sum_lag(run)
                    at(run, project, g, c)
                    at(tile + EMPTY_LAG, empty, g, c)
                    at(tile + SQUARE_LAG, square, g, c)
                    at(summed, sum_squares, g, c)
                at(summed + CHAIN_LAG, floor_sums, g)
                at(summed + 2 * CHAIN_LAG, invert_norms, g)
                at(summed + 3 * CHAIN_LAG, spread_norms, g)
                first = summed + 3 * CHAIN_LAG + APPLY_LAG
                for c in range(BLOCKS):
                    if g < DEFER_FROM[c // STREAM_BLOCKS]:
                        time = first + (c if g < GROUPS - 1 else c * FAST)
                        normalised[g, c] = min(time, max(first, STEPS) + (time - max(first, STEPS)) * FAST) if time > STEPS else time
            barrier = max(normalised[GROUPS - 1, c] for c in range(STREAM_BLOCKS)) + FAST + SQUARE_R_LAG
            for s in range(1, STREAMS):
                time = barrier + DEFER_LAG[s]
                for g in range(DEFER_FROM[s], GROUPS):
                    for c in range(s * STREAM_BLOCKS, (s + 1) * STREAM_BLOCKS):
                        normalised[g, c] = time
                        time += DEFER_PACE[s]
            free = 0
            for s in range(STREAMS):
                summed = 0
                for c in range(s * STREAM_BLOCKS, (s + 1) * STREAM_BLOCKS):
                    for g in range(GROUPS):
                        time = normalised[g, c]
                        at(time, normalise, g, c)
                        at(time + SQUARE_R_LAG, square_r, g, c)
                        summed = max(summed, time + SQUARE_R_LAG + FAST)
                for call, *args in statistics(s):
                    at(summed, call, *args)
                    summed += STAT_LAGS[s]
                first = max(free, summed)
                free = first + STORE_PACE * ROW_TILES
                for n in range(ROW_TILES):
                    g, j = n // GROUP_TILES, n % GROUP_TILES
                    c = s * STREAM_BLOCKS + j
                    if c not in TENSOR_SCALES:
                        at(first + STORE_PACE * max(n - 2.5, 0), scale_and_shift, g, c)
                    elif g == 0:
                        at(first, make_diagonal, c)
                    at(first + STORE_PACE * n + OUT_LAG, transpose_out, s, n)
                    at(first + STORE_PACE * n + OUT_LAG + LAND_LAG, land, s, n)
            with tc.manual_schedule():
                for time, n, call, args in sorted(calls, key=lambda entry: entry[:2]):
                    call(*args)
